import numpy as np
import ml_dtypes

BF16 = ml_dtypes.bfloat16


def bf(x):
    return np.asarray(x, np.float32).astype(BF16)


def f32(x):
    return np.asarray(x, np.float32)


def f64(x):
    return np.asarray(x).astype(np.float64)


def striped(idx):
    return np.tile(idx.reshape(-1, 16).T, (8, 1))


D, R, S, N = 128, 128, 4096, 2048
LN_EPS = 1e-5


def silu(v):
    return v / (1.0 + np.exp(-v))


def setup_inputs():
    return {
        "base": f32(np.random.standard_normal((D, S))),
        "wdot": f32(np.random.standard_normal((R, N))),
        "ln_gain": f32(1.0 + 0.1 * np.random.standard_normal((R, 1))),
        "ln_bias": f32(0.1 * np.random.standard_normal((R, 1))),
        "w_lin": bf(np.random.standard_normal((R, D)) / np.sqrt(R)),
        "b_lin": f32(0.1 * np.random.standard_normal((D, 1))),
        "tfeat": f32(np.random.standard_normal((D, N))),
        "w_t": bf(2.0 * np.random.standard_normal((D, D)) / np.sqrt(D)),
        "b_t": f32(0.1 * np.random.standard_normal((D, 1))),
        "offs": striped(np.random.permutation(S)[:N]),
    }


def reference(base, wdot, ln_gain, ln_bias, w_lin, b_lin, tfeat, w_t, b_t, offs):
    idx = offs[:16].T.reshape(-1)
    w = f64(wdot)
    mu = w.mean(axis=0, keepdims=True)
    var = ((w - mu) ** 2).mean(axis=0, keepdims=True)
    wn = (w - mu) / np.sqrt(var + LN_EPS) * f64(ln_gain) + f64(ln_bias)
    dw = f64(w_lin).T @ wn + f64(b_lin)
    t = f64(w_t).T @ silu(f64(tfeat)) + f64(b_t)
    out = f64(base).copy()
    out[:, idx] = dw * silu(t)
    return out

@@ -1,0 +1,110 @@
+import concourse.mybir as mybir
+
+F32 = mybir.dt.float32
+BF16 = mybir.dt.bfloat16
+U16 = mybir.dt.uint16
+ACT = mybir.ActivationFunctionType
+ALU = mybir.AluOpType
+
+P = 128
+S = 4096
+N = 2048
+CHUNK = 512
+PIECE = 1024
+LN_EPS = 1e-5
+FLOPS = 2 * 2 * P * P * N
+
+
+def tile_htr_kernel(tc, base, wdot, ln_gain, ln_bias, w_lin, b_lin, tfeat, w_t, b_t, offs, out):
+    nc = tc.nc
+    with (
+        tc.tile_pool(name="held", bufs=1) as held,
+        tc.tile_pool(name="loads", bufs=N // CHUNK) as loads,
+        tc.tile_pool(name="work", bufs=2) as work,
+        tc.tile_pool(name="factors", bufs=N // PIECE) as factors,
+        tc.psum_pool(name="psum", bufs=2) as psum,
+    ):
+        offsets = held.tile([P, N // 16], U16, name="offsets")
+        nc.sync.dma_start(offsets[:], offs)
+
+        wdot_chunks = []
+        tfeat_chunks = []
+        for c in range(N // CHUNK):
+            wdot_c = loads.tile([P, CHUNK], F32, name="wdot_c")
+            nc.sync.dma_start(wdot_c[:], wdot[:, c * CHUNK : (c + 1) * CHUNK])
+            wdot_chunks.append(wdot_c)
+            tfeat_c = loads.tile([P, CHUNK], F32, name="tfeat_c")
+            nc.sync.dma_start(tfeat_c[:], tfeat[:, c * CHUNK : (c + 1) * CHUNK])
+            tfeat_chunks.append(tfeat_c)
+
+        window = held.tile([P, S], F32, name="window")
+        nc.sync.dma_start(window[:], base)
+
+        w_lin_sb = held.tile([P, P], BF16, name="w_lin_sb")
+        nc.scalar.dma_start(w_lin_sb[:], w_lin)
+        w_t_sb = held.tile([P, P], BF16, name="w_t_sb")
+        nc.scalar.dma_start(w_t_sb[:], w_t)
+        gain_col = held.tile([P, 1], F32, name="gain_col")
+        nc.scalar.dma_start(gain_col[:], ln_gain)
+        bias_col = held.tile([P, 1], F32, name="bias_col")
+        nc.scalar.dma_start(bias_col[:], ln_bias)
+        b_lin_col = held.tile([P, 1], F32, name="b_lin_col")
+        nc.scalar.dma_start(b_lin_col[:], b_lin)
+        b_t_col = held.tile([P, 1], F32, name="b_t_col")
+        nc.scalar.dma_start(b_t_col[:], b_t)
+
+        centre = held.tile([P, P], F32, name="centre")
+        nc.gpsimd.memset(centre[:], -1.0 / P)
+        nc.gpsimd.affine_select(
+            out=centre[:],
+            in_=centre[:],
+            compare_op=ALU.not_equal,
+            fill=1.0 - 1.0 / P,
+            base=0,
+            pattern=[[-1, P]],
+            channel_multiplier=1,
+        )
+        average = held.tile([P, P], F32, name="average")
+        nc.gpsimd.memset(average[:], 1.0 / P)
+        minus_half = held.tile([P, CHUNK], F32, name="minus_half")
+        nc.gpsimd.memset(minus_half[:], -0.5)
+
+        for piece in range(N // PIECE):
+            dw = factors.tile([P, PIECE], F32, name="dw")
+            gate = factors.tile([P, PIECE], F32, name="gate")
+            for half in range(PIECE // CHUNK):
+                c = piece * (PIECE // CHUNK) + half
+                cols = slice(half * CHUNK, (half + 1) * CHUNK)
+
+                act_feat = work.tile([P, CHUNK], BF16, name="act_feat")
+                nc.scalar.activation(act_feat[:], tfeat_chunks[c][:], ACT.Silu)
+                t_ps = psum.tile([P, CHUNK], F32, name="t_ps")
+                nc.tensor.matmul(t_ps[:], w_t_sb[:], act_feat[:], start=True, stop=True)
+                nc.scalar.activation(gate[:, cols], t_ps[:], ACT.Silu, bias=b_t_col[:, 0:1])
+
+                centred_ps = psum.tile([P, CHUNK], F32, name="centred_ps")
+                nc.tensor.matmul(centred_ps[:], centre[:], wdot_chunks[c][:], start=True, stop=True)
+                squared = work.tile([P, CHUNK], F32, name="squared")
+                nc.scalar.activation(squared[:], centred_ps[:], ACT.Square)
+                var_ps = psum.tile([P, CHUNK], F32, name="var_ps")
+                nc.tensor.matmul(var_ps[:], average[:], squared[:], start=True, stop=True)
+                var_eps = work.tile([P, CHUNK], F32, name="var_eps")
+                nc.vector.tensor_scalar_add(var_eps[:], var_ps[:], LN_EPS)
+                rstd = work.tile([P, CHUNK], F32, name="rstd")
+                nc.gpsimd.tensor_tensor(rstd[:], var_eps[:], minus_half[:], ALU.pow)
+                scaled = work.tile([P, CHUNK], F32, name="scaled")
+                nc.vector.tensor_tensor(scaled[:], centred_ps[:], rstd[:], ALU.mult)
+                normed = work.tile([P, CHUNK], BF16, name="normed")
+                nc.vector.tensor_scalar(
+                    normed[:], scaled[:], gain_col[:, 0:1], bias_col[:, 0:1], ALU.mult, ALU.add
+                )
+
+                dw_ps = psum.tile([P, CHUNK], F32, name="dw_ps")
+                nc.tensor.matmul(dw_ps[:], w_lin_sb[:], normed[:], start=True, stop=True)
+                nc.scalar.activation(dw[:, cols], dw_ps[:], ACT.Identity, bias=b_lin_col[:, 0:1])
+
+            piece_offsets = offsets[:, piece * (PIECE // 16) : (piece + 1) * (PIECE // 16)]
+            nc.vector.tensor_tensor(window[:].indirect(piece_offsets), dw[:], gate[:], ALU.mult)
+
+        nc.sync.dma_start(out[:, 0 : S // 2], window[:, 0 : S // 2])
+        nc.scalar.dma_start(out[:, S // 2 : S], window[:, S // 2 : S])

@@ -9,50 +9,54 @@ ALU = mybir.AluOpType
 P = 128
 S = 4096
 N = 2048
-CHUNK = 512
+LOAD = 512
+CHUNK = 256
 PIECE = 1024
+CHUNKS = N // CHUNK
 LN_EPS = 1e-5
 FLOPS = 2 * 2 * P * P * N
+WARM_UP = 4
 
 
 def tile_htr_kernel(tc, base, wdot, ln_gain, ln_bias, w_lin, b_lin, tfeat, w_t, b_t, offs, out):
     nc = tc.nc
+    per_piece = PIECE // CHUNK
+
+    def chunk_of(loaded, c):
+        first = c * CHUNK
+        return loaded[first // LOAD][:, first % LOAD : first % LOAD + CHUNK]
+
+    def chunk_in_piece(factor, c):
+        first = (c % per_piece) * CHUNK
+        return factor[c // per_piece][:, first : first + CHUNK]
+
     with (
         tc.tile_pool(name="held", bufs=1) as held,
-        tc.tile_pool(name="loads", bufs=N // CHUNK) as loads,
-        tc.tile_pool(name="work", bufs=2) as work,
-        tc.tile_pool(name="factors", bufs=N // PIECE) as factors,
+        tc.tile_pool(name="chunked", bufs=CHUNKS) as chunked,
         tc.psum_pool(name="psum", bufs=2) as psum,
     ):
+        tfeat_sb = [held.tile([P, LOAD], F32, name=f"tfeat_sb{i}") for i in range(N // LOAD)]
+        wdot_sb = [held.tile([P, LOAD], F32, name=f"wdot_sb{i}") for i in range(N // LOAD)]
+        b_lin_col = held.tile([P, 1], F32, name="b_lin_col")
         offsets = held.tile([P, N // 16], U16, name="offsets")
-        nc.sync.dma_start(offsets[:], offs)
-
-        wdot_chunks = []
-        tfeat_chunks = []
-        for c in range(N // CHUNK):
-            wdot_c = loads.tile([P, CHUNK], F32, name="wdot_c")
-            nc.sync.dma_start(wdot_c[:], wdot[:, c * CHUNK : (c + 1) * CHUNK])
-            wdot_chunks.append(wdot_c)
-            tfeat_c = loads.tile([P, CHUNK], F32, name="tfeat_c")
-            nc.sync.dma_start(tfeat_c[:], tfeat[:, c * CHUNK : (c + 1) * CHUNK])
-            tfeat_chunks.append(tfeat_c)
-
         window = held.tile([P, S], F32, name="window")
+        for i in range(N // LOAD):
+            nc.sync.dma_start(tfeat_sb[i][:], tfeat[:, i * LOAD : (i + 1) * LOAD])
+        for i in range(N // LOAD):
+            nc.sync.dma_start(wdot_sb[i][:], wdot[:, i * LOAD : (i + 1) * LOAD])
+        nc.sync.dma_start(b_lin_col[:], b_lin)
+        nc.sync.dma_start(offsets[:], offs)
         nc.sync.dma_start(window[:], base)
 
-        w_lin_sb = held.tile([P, P], BF16, name="w_lin_sb")
-        nc.scalar.dma_start(w_lin_sb[:], w_lin)
         w_t_sb = held.tile([P, P], BF16, name="w_t_sb")
         nc.scalar.dma_start(w_t_sb[:], w_t)
-        gain_col = held.tile([P, 1], F32, name="gain_col")
-        nc.scalar.dma_start(gain_col[:], ln_gain)
-        bias_col = held.tile([P, 1], F32, name="bias_col")
-        nc.scalar.dma_start(bias_col[:], ln_bias)
-        b_lin_col = held.tile([P, 1], F32, name="b_lin_col")
-        nc.scalar.dma_start(b_lin_col[:], b_lin)
         b_t_col = held.tile([P, 1], F32, name="b_t_col")
         nc.scalar.dma_start(b_t_col[:], b_t)
 
+        average = held.tile([P, P], F32, name="average")
+        nc.vector.memset(average[:], 1.0 / P)
+        eps_col = held.tile([P, 1], F32, name="eps_col")
+        nc.vector.memset(eps_col[:], LN_EPS)
         centre = held.tile([P, P], F32, name="centre")
         nc.gpsimd.memset(centre[:], -1.0 / P)
         nc.gpsimd.affine_select(
@@ -64,47 +68,58 @@ def tile_htr_kernel(tc, base, wdot, ln_gain, ln_bias, w_lin, b_lin, tfeat, w_t, 
             pattern=[[-1, P]],
             channel_multiplier=1,
         )
-        average = held.tile([P, P], F32, name="average")
-        nc.gpsimd.memset(average[:], 1.0 / P)
-        minus_half = held.tile([P, CHUNK], F32, name="minus_half")
-        nc.gpsimd.memset(minus_half[:], -0.5)
 
+        gain_col = held.tile([P, 1], F32, name="gain_col")
+        nc.gpsimd.dma_start(gain_col[:], ln_gain)
+        bias_col = held.tile([P, 1], F32, name="bias_col")
+        nc.gpsimd.dma_start(bias_col[:], ln_bias)
+        w_lin_sb = held.tile([P, P], BF16, name="w_lin_sb")
+        nc.gpsimd.dma_start(w_lin_sb[:], w_lin)
+
+        table_warmer = held.tile([P, 1], F32, name="table_warmer")
+        nc.scalar.activation(table_warmer[:], eps_col[:], ACT.Silu)
+        idle_ps = psum.tile([P, P], F32, name="idle_ps", tag="t_or_dw")
+        for i in range(WARM_UP):
+            nc.tensor.matmul(idle_ps[:], average[:], average[:], start=True, stop=True)
+
+        gates = [held.tile([P, PIECE], F32, name=f"gate{piece}") for piece in range(N // PIECE)]
+        for c in range(CHUNKS):
+            act_feat = chunked.tile([P, CHUNK], BF16, name="act_feat")
+            nc.scalar.activation(act_feat[:], chunk_of(tfeat_sb, c), ACT.Silu)
+            t_ps = psum.tile([P, CHUNK], F32, name="t_ps", tag="t_or_dw")
+            nc.tensor.matmul(t_ps[:], w_t_sb[:], act_feat[:], start=True, stop=True)
+            nc.scalar.activation(chunk_in_piece(gates, c), t_ps[:], ACT.Silu, bias=b_t_col[:, 0:1])
+
+        dws = [held.tile([P, PIECE], F32, name=f"dw{piece}") for piece in range(N // PIECE)]
         for piece in range(N // PIECE):
-            dw = factors.tile([P, PIECE], F32, name="dw")
-            gate = factors.tile([P, PIECE], F32, name="gate")
-            for half in range(PIECE // CHUNK):
-                c = piece * (PIECE // CHUNK) + half
-                cols = slice(half * CHUNK, (half + 1) * CHUNK)
-
-                act_feat = work.tile([P, CHUNK], BF16, name="act_feat")
-                nc.scalar.activation(act_feat[:], tfeat_chunks[c][:], ACT.Silu)
-                t_ps = psum.tile([P, CHUNK], F32, name="t_ps")
-                nc.tensor.matmul(t_ps[:], w_t_sb[:], act_feat[:], start=True, stop=True)
-                nc.scalar.activation(gate[:, cols], t_ps[:], ACT.Silu, bias=b_t_col[:, 0:1])
-
+            vector_is_free = piece == 0
+            elementwise = nc.vector if vector_is_free else nc.gpsimd
+            for c in range(piece * per_piece, (piece + 1) * per_piece):
                 centred_ps = psum.tile([P, CHUNK], F32, name="centred_ps")
-                nc.tensor.matmul(centred_ps[:], centre[:], wdot_chunks[c][:], start=True, stop=True)
-                squared = work.tile([P, CHUNK], F32, name="squared")
-                nc.scalar.activation(squared[:], centred_ps[:], ACT.Square)
-                var_ps = psum.tile([P, CHUNK], F32, name="var_ps")
+                nc.tensor.matmul(centred_ps[:], centre[:], chunk_of(wdot_sb, c), start=True, stop=True)
+                centred = chunked.tile([P, CHUNK], F32, name="centred")
+                squared = chunked.tile([P, CHUNK], F32, name="squared")
+                if vector_is_free:
+                    nc.vector.tensor_copy(centred[:], centred_ps[:])
+                    nc.vector.tensor_tensor(squared[:], centred[:], centred_ps[:], ALU.mult)
+                else:
+                    nc.scalar.activation(squared[:], centred_ps[:], ACT.Square)
+                    nc.scalar.activation(centred[:], centred_ps[:], ACT.Copy)
+                var_ps = psum.tile([P, CHUNK], F32, name="var_ps", bufs=per_piece)
                 nc.tensor.matmul(var_ps[:], average[:], squared[:], start=True, stop=True)
-                var_eps = work.tile([P, CHUNK], F32, name="var_eps")
-                nc.vector.tensor_scalar_add(var_eps[:], var_ps[:], LN_EPS)
-                rstd = work.tile([P, CHUNK], F32, name="rstd")
-                nc.gpsimd.tensor_tensor(rstd[:], var_eps[:], minus_half[:], ALU.pow)
-                scaled = work.tile([P, CHUNK], F32, name="scaled")
-                nc.vector.tensor_tensor(scaled[:], centred_ps[:], rstd[:], ALU.mult)
-                normed = work.tile([P, CHUNK], BF16, name="normed")
-                nc.vector.tensor_scalar(
-                    normed[:], scaled[:], gain_col[:, 0:1], bias_col[:, 0:1], ALU.mult, ALU.add
-                )
+                rstd = chunked.tile([P, CHUNK], F32, name="rstd")
+                nc.scalar.activation(rstd[:], var_ps[:], ACT.Abs_reciprocal_sqrt, bias=eps_col[:, 0:1])
+                scaled = chunked.tile([P, CHUNK], F32, name="scaled")
+                elementwise.tensor_tensor(scaled[:], centred[:], rstd[:], ALU.mult)
+                normed = chunked.tile([P, CHUNK], BF16, name="normed")
+                elementwise.tensor_scalar(normed[:], scaled[:], gain_col[:, 0:1], bias_col[:, 0:1], ALU.mult, ALU.add)
 
-                dw_ps = psum.tile([P, CHUNK], F32, name="dw_ps")
+                dw_ps = psum.tile([P, CHUNK], F32, name="dw_ps", tag="t_or_dw")
                 nc.tensor.matmul(dw_ps[:], w_lin_sb[:], normed[:], start=True, stop=True)
-                nc.scalar.activation(dw[:, cols], dw_ps[:], ACT.Identity, bias=b_lin_col[:, 0:1])
+                nc.scalar.activation(chunk_in_piece(dws, c), dw_ps[:], ACT.Identity, bias=b_lin_col[:, 0:1])
 
             piece_offsets = offsets[:, piece * (PIECE // 16) : (piece + 1) * (PIECE // 16)]
-            nc.vector.tensor_tensor(window[:].indirect(piece_offsets), dw[:], gate[:], ALU.mult)
+            nc.vector.tensor_tensor(window[:].indirect(piece_offsets), dws[piece][:], gates[piece][:], ALU.mult)
 
         nc.sync.dma_start(out[:, 0 : S // 2], window[:, 0 : S // 2])
         nc.scalar.dma_start(out[:, S // 2 : S], window[:, S // 2 : S])

@@ -15,7 +15,6 @@ PIECE = 1024
 CHUNKS = N // CHUNK
 LN_EPS = 1e-5
 FLOPS = 2 * 2 * P * P * N
-WARM_UP = 4
 
 
 def tile_htr_kernel(tc, base, wdot, ln_gain, ln_bias, w_lin, b_lin, tfeat, w_t, b_t, offs, out):
@@ -78,9 +77,6 @@ def tile_htr_kernel(tc, base, wdot, ln_gain, ln_bias, w_lin, b_lin, tfeat, w_t, 
 
         table_warmer = held.tile([P, 1], F32, name="table_warmer")
         nc.scalar.activation(table_warmer[:], eps_col[:], ACT.Silu)
-        idle_ps = psum.tile([P, P], F32, name="idle_ps", tag="t_or_dw")
-        for i in range(WARM_UP):
-            nc.tensor.matmul(idle_ps[:], average[:], average[:], start=True, stop=True)
 
         gates = [held.tile([P, PIECE], F32, name=f"gate{piece}") for piece in range(N // PIECE)]
         for c in range(CHUNKS):

@@ -9,17 +9,20 @@ ALU = mybir.AluOpType
 P = 128
 S = 4096
 N = 2048
-LOAD = 512
+LOAD = 1024
 CHUNK = 256
 PIECE = 1024
 CHUNKS = N // CHUNK
 LN_EPS = 1e-5
 FLOPS = 2 * 2 * P * P * N
+WARM_UP = 4
 
 
 def tile_htr_kernel(tc, base, wdot, ln_gain, ln_bias, w_lin, b_lin, tfeat, w_t, b_t, offs, out):
     nc = tc.nc
     per_piece = PIECE // CHUNK
+    first_piece = range(per_piece)
+    second_piece = range(per_piece, CHUNKS)
 
     def chunk_of(loaded, c):
         first = c * CHUNK
@@ -36,21 +39,27 @@ def tile_htr_kernel(tc, base, wdot, ln_gain, ln_bias, w_lin, b_lin, tfeat, w_t, 
     ):
         tfeat_sb = [held.tile([P, LOAD], F32, name=f"tfeat_sb{i}") for i in range(N // LOAD)]
         wdot_sb = [held.tile([P, LOAD], F32, name=f"wdot_sb{i}") for i in range(N // LOAD)]
+        w_t_sb = held.tile([P, P], BF16, name="w_t_sb")
+        w_lin_sb = held.tile([P, P], BF16, name="w_lin_sb")
+        b_t_col = held.tile([P, 1], F32, name="b_t_col")
+        gain_col = held.tile([P, 1], F32, name="gain_col")
+        bias_col = held.tile([P, 1], F32, name="bias_col")
         b_lin_col = held.tile([P, 1], F32, name="b_lin_col")
         offsets = held.tile([P, N // 16], U16, name="offsets")
         window = held.tile([P, S], F32, name="window")
-        for i in range(N // LOAD):
-            nc.sync.dma_start(tfeat_sb[i][:], tfeat[:, i * LOAD : (i + 1) * LOAD])
-        for i in range(N // LOAD):
-            nc.sync.dma_start(wdot_sb[i][:], wdot[:, i * LOAD : (i + 1) * LOAD])
+
+        nc.scalar.dma_start(w_t_sb[:], w_t)
+        nc.scalar.dma_start(b_t_col[:], b_t)
+        nc.sync.dma_start(tfeat_sb[0][:], tfeat[:, 0:LOAD])
+        nc.scalar.dma_start(wdot_sb[0][:], wdot[:, 0:LOAD])
+        nc.sync.dma_start(tfeat_sb[1][:], tfeat[:, LOAD : 2 * LOAD])
+        nc.sync.dma_start(gain_col[:], ln_gain)
+        nc.sync.dma_start(bias_col[:], ln_bias)
+        nc.scalar.dma_start(wdot_sb[1][:], wdot[:, LOAD : 2 * LOAD])
+        nc.sync.dma_start(w_lin_sb[:], w_lin)
         nc.sync.dma_start(b_lin_col[:], b_lin)
         nc.sync.dma_start(offsets[:], offs)
         nc.sync.dma_start(window[:], base)
-
-        w_t_sb = held.tile([P, P], BF16, name="w_t_sb")
-        nc.scalar.dma_start(w_t_sb[:], w_t)
-        b_t_col = held.tile([P, 1], F32, name="b_t_col")
-        nc.scalar.dma_start(b_t_col[:], b_t)
 
         average = held.tile([P, P], F32, name="average")
         nc.vector.memset(average[:], 1.0 / P)
@@ -68,54 +77,80 @@ def tile_htr_kernel(tc, base, wdot, ln_gain, ln_bias, w_lin, b_lin, tfeat, w_t, 
             channel_multiplier=1,
         )
 
-        gain_col = held.tile([P, 1], F32, name="gain_col")
-        nc.gpsimd.dma_start(gain_col[:], ln_gain)
-        bias_col = held.tile([P, 1], F32, name="bias_col")
-        nc.gpsimd.dma_start(bias_col[:], ln_bias)
-        w_lin_sb = held.tile([P, P], BF16, name="w_lin_sb")
-        nc.gpsimd.dma_start(w_lin_sb[:], w_lin)
-
         table_warmer = held.tile([P, 1], F32, name="table_warmer")
         nc.scalar.activation(table_warmer[:], eps_col[:], ACT.Silu)
+        idle_ps = psum.tile([P, P], F32, name="idle_ps", tag="t_or_dw")
+        for i in range(WARM_UP):
+            nc.tensor.matmul(idle_ps[:], average[:], average[:], start=True, stop=True)
 
         gates = [held.tile([P, PIECE], F32, name=f"gate{piece}") for piece in range(N // PIECE)]
-        for c in range(CHUNKS):
+        dws = [held.tile([P, PIECE], F32, name=f"dw{piece}") for piece in range(N // PIECE)]
+        centred, squared = {}, {}
+
+        def gate(c):
             act_feat = chunked.tile([P, CHUNK], BF16, name="act_feat")
             nc.scalar.activation(act_feat[:], chunk_of(tfeat_sb, c), ACT.Silu)
             t_ps = psum.tile([P, CHUNK], F32, name="t_ps", tag="t_or_dw")
             nc.tensor.matmul(t_ps[:], w_t_sb[:], act_feat[:], start=True, stop=True)
             nc.scalar.activation(chunk_in_piece(gates, c), t_ps[:], ACT.Silu, bias=b_t_col[:, 0:1])
 
-        dws = [held.tile([P, PIECE], F32, name=f"dw{piece}") for piece in range(N // PIECE)]
-        for piece in range(N // PIECE):
-            vector_is_free = piece == 0
-            elementwise = nc.vector if vector_is_free else nc.gpsimd
-            for c in range(piece * per_piece, (piece + 1) * per_piece):
-                centred_ps = psum.tile([P, CHUNK], F32, name="centred_ps")
-                nc.tensor.matmul(centred_ps[:], centre[:], chunk_of(wdot_sb, c), start=True, stop=True)
-                centred = chunked.tile([P, CHUNK], F32, name="centred")
-                squared = chunked.tile([P, CHUNK], F32, name="squared")
-                if vector_is_free:
-                    nc.vector.tensor_copy(centred[:], centred_ps[:])
-                    nc.vector.tensor_tensor(squared[:], centred[:], centred_ps[:], ALU.mult)
-                else:
-                    nc.scalar.activation(squared[:], centred_ps[:], ACT.Square)
-                    nc.scalar.activation(centred[:], centred_ps[:], ACT.Copy)
-                var_ps = psum.tile([P, CHUNK], F32, name="var_ps", bufs=per_piece)
-                nc.tensor.matmul(var_ps[:], average[:], squared[:], start=True, stop=True)
-                rstd = chunked.tile([P, CHUNK], F32, name="rstd")
-                nc.scalar.activation(rstd[:], var_ps[:], ACT.Abs_reciprocal_sqrt, bias=eps_col[:, 0:1])
-                scaled = chunked.tile([P, CHUNK], F32, name="scaled")
-                elementwise.tensor_tensor(scaled[:], centred[:], rstd[:], ALU.mult)
-                normed = chunked.tile([P, CHUNK], BF16, name="normed")
-                elementwise.tensor_scalar(normed[:], scaled[:], gain_col[:, 0:1], bias_col[:, 0:1], ALU.mult, ALU.add)
+        def centre_and_square(c, vector_is_free):
+            centred_ps = psum.tile([P, CHUNK], F32, name="centred_ps")
+            nc.tensor.matmul(centred_ps[:], centre[:], chunk_of(wdot_sb, c), start=True, stop=True)
+            centred[c] = chunked.tile([P, CHUNK], F32, name="centred")
+            squared[c] = chunked.tile([P, CHUNK], F32, name="squared")
+            if vector_is_free:
+                nc.vector.tensor_copy(centred[c][:], centred_ps[:])
+                nc.vector.tensor_tensor(squared[c][:], centred[c][:], centred_ps[:], ALU.mult)
+            else:
+                nc.scalar.activation(squared[c][:], centred_ps[:], ACT.Square)
+                nc.scalar.activation(centred[c][:], centred_ps[:], ACT.Copy)
 
-                dw_ps = psum.tile([P, CHUNK], F32, name="dw_ps", tag="t_or_dw")
-                nc.tensor.matmul(dw_ps[:], w_lin_sb[:], normed[:], start=True, stop=True)
-                nc.scalar.activation(chunk_in_piece(dws, c), dw_ps[:], ACT.Identity, bias=b_lin_col[:, 0:1])
+        var_ps, normed, dw_ps = {}, {}, {}
 
+        def mean_of_squares(c):
+            var_ps[c] = psum.tile([P, CHUNK], F32, name="var_ps", bufs=per_piece)
+            nc.tensor.matmul(var_ps[c][:], average[:], squared[c][:], start=True, stop=True)
+
+        def normalise(c, elementwise):
+            rstd = chunked.tile([P, CHUNK], F32, name="rstd")
+            nc.scalar.activation(rstd[:], var_ps[c][:], ACT.Abs_reciprocal_sqrt, bias=eps_col[:, 0:1])
+            scaled = chunked.tile([P, CHUNK], F32, name="scaled")
+            elementwise.tensor_tensor(scaled[:], centred[c][:], rstd[:], ALU.mult)
+            normed[c] = chunked.tile([P, CHUNK], BF16, name="normed")
+            elementwise.tensor_scalar(normed[c][:], scaled[:], gain_col[:, 0:1], bias_col[:, 0:1], ALU.mult, ALU.add)
+
+        def linear(c):
+            dw_ps[c] = psum.tile([P, CHUNK], F32, name="dw_ps", tag="t_or_dw")
+            nc.tensor.matmul(dw_ps[c][:], w_lin_sb[:], normed[c][:], start=True, stop=True)
+            nc.scalar.activation(chunk_in_piece(dws, c), dw_ps[c][:], ACT.Identity, bias=b_lin_col[:, 0:1])
+
+        def place(piece):
             piece_offsets = offsets[:, piece * (PIECE // 16) : (piece + 1) * (PIECE // 16)]
             nc.vector.tensor_tensor(window[:].indirect(piece_offsets), dws[piece][:], gates[piece][:], ALU.mult)
+
+        for c in first_piece:
+            gate(c)
+        for c in first_piece:
+            centre_and_square(c, True)
+        for c in second_piece:
+            gate(c)
+        for c in first_piece:
+            mean_of_squares(c)
+        for c in first_piece:
+            normalise(c, nc.vector)
+        for c in first_piece:
+            linear(c)
+        place(0)
+        for c in second_piece:
+            centre_and_square(c, False)
+        for c in second_piece:
+            mean_of_squares(c)
+        for c in second_piece:
+            normalise(c, nc.gpsimd)
+        for c in second_piece:
+            linear(c)
+        place(1)
 
         nc.sync.dma_start(out[:, 0 : S // 2], window[:, 0 : S // 2])
         nc.scalar.dma_start(out[:, S // 2 : S], window[:, S // 2 : S])

@@ -35,7 +35,7 @@ def tile_htr_kernel(tc, base, wdot, ln_gain, ln_bias, w_lin, b_lin, tfeat, w_t, 
     with (
         tc.tile_pool(name="held", bufs=1) as held,
         tc.tile_pool(name="chunked", bufs=CHUNKS) as chunked,
-        tc.psum_pool(name="psum", bufs=2) as psum,
+        tc.psum_pool(name="psum", bufs=3) as psum,
     ):
         tfeat_sb = [held.tile([P, LOAD], F32, name=f"tfeat_sb{i}") for i in range(N // LOAD)]
         wdot_sb = [held.tile([P, LOAD], F32, name=f"wdot_sb{i}") for i in range(N // LOAD)]
@@ -79,23 +79,25 @@ def tile_htr_kernel(tc, base, wdot, ln_gain, ln_bias, w_lin, b_lin, tfeat, w_t, 
 
         table_warmer = held.tile([P, 1], F32, name="table_warmer")
         nc.scalar.activation(table_warmer[:], eps_col[:], ACT.Silu)
-        idle_ps = psum.tile([P, P], F32, name="idle_ps", tag="t_or_dw")
+        idle_ps = psum.tile([P, P], F32, name="idle_ps", tag="t_or_dw", bufs=2)
         for i in range(WARM_UP):
             nc.tensor.matmul(idle_ps[:], average[:], average[:], start=True, stop=True)
 
         gates = [held.tile([P, PIECE], F32, name=f"gate{piece}") for piece in range(N // PIECE)]
         dws = [held.tile([P, PIECE], F32, name=f"dw{piece}") for piece in range(N // PIECE)]
         centred, squared = {}, {}
+        banks_of_centred = ["norm_a", "norm_b"]
+        banks_of_var = ["norm_b", "norm_a"]
 
         def gate(c):
             act_feat = chunked.tile([P, CHUNK], BF16, name="act_feat")
             nc.scalar.activation(act_feat[:], chunk_of(tfeat_sb, c), ACT.Silu)
-            t_ps = psum.tile([P, CHUNK], F32, name="t_ps", tag="t_or_dw")
+            t_ps = psum.tile([P, CHUNK], F32, name="t_ps", tag="t_or_dw", bufs=2)
             nc.tensor.matmul(t_ps[:], w_t_sb[:], act_feat[:], start=True, stop=True)
             nc.scalar.activation(chunk_in_piece(gates, c), t_ps[:], ACT.Silu, bias=b_t_col[:, 0:1])
 
         def centre_and_square(c, vector_is_free):
-            centred_ps = psum.tile([P, CHUNK], F32, name="centred_ps")
+            centred_ps = psum.tile([P, CHUNK], F32, name="centred_ps", tag=banks_of_centred[c // per_piece])
             nc.tensor.matmul(centred_ps[:], centre[:], chunk_of(wdot_sb, c), start=True, stop=True)
             centred[c] = chunked.tile([P, CHUNK], F32, name="centred")
             squared[c] = chunked.tile([P, CHUNK], F32, name="squared")
@@ -106,23 +108,30 @@ def tile_htr_kernel(tc, base, wdot, ln_gain, ln_bias, w_lin, b_lin, tfeat, w_t, 
                 nc.scalar.activation(squared[c][:], centred_ps[:], ACT.Square)
                 nc.scalar.activation(centred[c][:], centred_ps[:], ACT.Copy)
 
-        var_ps, normed, dw_ps = {}, {}, {}
+        var_ps, dw_ps = {}, {}
 
         def mean_of_squares(c):
-            var_ps[c] = psum.tile([P, CHUNK], F32, name="var_ps", bufs=per_piece)
+            var_ps[c] = psum.tile([P, CHUNK], F32, name="var_ps", tag=banks_of_var[c // per_piece])
             nc.tensor.matmul(var_ps[c][:], average[:], squared[c][:], start=True, stop=True)
 
-        def normalise(c, elementwise):
+        scaled = {}
+
+        def scale_by_root(c, multiplier):
             rstd = chunked.tile([P, CHUNK], F32, name="rstd")
             nc.scalar.activation(rstd[:], var_ps[c][:], ACT.Abs_reciprocal_sqrt, bias=eps_col[:, 0:1])
-            scaled = chunked.tile([P, CHUNK], F32, name="scaled")
-            elementwise.tensor_tensor(scaled[:], centred[c][:], rstd[:], ALU.mult)
-            normed[c] = chunked.tile([P, CHUNK], BF16, name="normed")
-            elementwise.tensor_scalar(normed[c][:], scaled[:], gain_col[:, 0:1], bias_col[:, 0:1], ALU.mult, ALU.add)
+            scaled[c] = chunked.tile([P, CHUNK], F32, name="scaled")
+            multiplier.tensor_tensor(scaled[c][:], centred[c][:], rstd[:], ALU.mult)
 
-        def linear(c):
-            dw_ps[c] = psum.tile([P, CHUNK], F32, name="dw_ps", tag="t_or_dw")
-            nc.tensor.matmul(dw_ps[c][:], w_lin_sb[:], normed[c][:], start=True, stop=True)
+        def linear(c, vector_is_free):
+            normed = chunked.tile([P, CHUNK], BF16, name="normed")
+            if vector_is_free:
+                nc.vector.tensor_scalar(normed[:], scaled[c][:], gain_col[:, 0:1], bias_col[:, 0:1], ALU.mult, ALU.add)
+            else:
+                nc.scalar.activation(normed[:], scaled[c][:], ACT.Identity, bias=bias_col[:, 0:1], scale=gain_col[:, 0:1])
+            dw_ps[c] = psum.tile([P, CHUNK], F32, name="dw_ps", tag="t_or_dw", bufs=2)
+            nc.tensor.matmul(dw_ps[c][:], w_lin_sb[:], normed[:], start=True, stop=True)
+
+        def add_b_lin(c):
             nc.scalar.activation(chunk_in_piece(dws, c), dw_ps[c][:], ACT.Identity, bias=b_lin_col[:, 0:1])
 
         def place(piece):
@@ -138,18 +147,23 @@ def tile_htr_kernel(tc, base, wdot, ln_gain, ln_bias, w_lin, b_lin, tfeat, w_t, 
         for c in first_piece:
             mean_of_squares(c)
         for c in first_piece:
-            normalise(c, nc.vector)
+            scale_by_root(c, nc.vector)
         for c in first_piece:
-            linear(c)
+            linear(c, True)
+        for c in first_piece:
+            add_b_lin(c)
         place(0)
-        for c in second_piece:
-            centre_and_square(c, False)
-        for c in second_piece:
-            mean_of_squares(c)
-        for c in second_piece:
-            normalise(c, nc.gpsimd)
-        for c in second_piece:
-            linear(c)
+        for round_no in range(per_piece + 3):
+            oldest = per_piece + round_no - 3
+            if oldest in second_piece:
+                add_b_lin(oldest)
+            if oldest + 1 in second_piece:
+                linear(oldest + 1, False)
+            if oldest + 2 in second_piece:
+                mean_of_squares(oldest + 2)
+                scale_by_root(oldest + 2, nc.gpsimd)
+            if oldest + 3 in second_piece:
+                centre_and_square(oldest + 3, False)
         place(1)
 
         nc.sync.dma_start(out[:, 0 : S // 2], window[:, 0 : S // 2])

@@ -15,7 +15,6 @@ PIECE = 1024
 CHUNKS = N // CHUNK
 LN_EPS = 1e-5
 FLOPS = 2 * 2 * P * P * N
-WARM_UP = 4
 
 
 def tile_htr_kernel(tc, base, wdot, ln_gain, ln_bias, w_lin, b_lin, tfeat, w_t, b_t, offs, out):
@@ -79,9 +78,6 @@ def tile_htr_kernel(tc, base, wdot, ln_gain, ln_bias, w_lin, b_lin, tfeat, w_t, 
 
         table_warmer = held.tile([P, 1], F32, name="table_warmer")
         nc.scalar.activation(table_warmer[:], eps_col[:], ACT.Silu)
-        idle_ps = psum.tile([P, P], F32, name="idle_ps", tag="t_or_dw", bufs=2)
-        for i in range(WARM_UP):
-            nc.tensor.matmul(idle_ps[:], average[:], average[:], start=True, stop=True)
 
         gates = [held.tile([P, PIECE], F32, name=f"gate{piece}") for piece in range(N // PIECE)]
         dws = [held.tile([P, PIECE], F32, name=f"dw{piece}") for piece in range(N // PIECE)]

@@ -11,8 +11,9 @@ S = 4096
 N = 2048
 LOAD = 1024
 CHUNK = 256
-PIECE = 1024
+PIECE = 512
 CHUNKS = N // CHUNK
+PIECES = N // PIECE
 LN_EPS = 1e-5
 FLOPS = 2 * 2 * P * P * N
 
@@ -20,8 +21,9 @@ FLOPS = 2 * 2 * P * P * N
 def tile_htr_kernel(tc, base, wdot, ln_gain, ln_bias, w_lin, b_lin, tfeat, w_t, b_t, offs, out):
     nc = tc.nc
     per_piece = PIECE // CHUNK
-    first_piece = range(per_piece)
-    second_piece = range(per_piece, CHUNKS)
+
+    def chunks_of(piece):
+        return range(piece * per_piece, (piece + 1) * per_piece)
 
     def chunk_of(loaded, c):
         first = c * CHUNK
@@ -34,7 +36,7 @@ def tile_htr_kernel(tc, base, wdot, ln_gain, ln_bias, w_lin, b_lin, tfeat, w_t, 
     with (
         tc.tile_pool(name="held", bufs=1) as held,
         tc.tile_pool(name="chunked", bufs=CHUNKS) as chunked,
-        tc.psum_pool(name="psum", bufs=3) as psum,
+        tc.psum_pool(name="psum", bufs=2) as psum,
     ):
         tfeat_sb = [held.tile([P, LOAD], F32, name=f"tfeat_sb{i}") for i in range(N // LOAD)]
         wdot_sb = [held.tile([P, LOAD], F32, name=f"wdot_sb{i}") for i in range(N // LOAD)]
@@ -47,18 +49,18 @@ def tile_htr_kernel(tc, base, wdot, ln_gain, ln_bias, w_lin, b_lin, tfeat, w_t, 
         offsets = held.tile([P, N // 16], U16, name="offsets")
         window = held.tile([P, S], F32, name="window")
 
-        nc.scalar.dma_start(w_t_sb[:], w_t)
-        nc.scalar.dma_start(b_t_col[:], b_t)
+        nc.sync.dma_start(w_t_sb[:], w_t)
+        nc.sync.dma_start(b_t_col[:], b_t)
         nc.sync.dma_start(tfeat_sb[0][:], tfeat[:, 0:LOAD])
-        nc.scalar.dma_start(wdot_sb[0][:], wdot[:, 0:LOAD])
+        nc.sync.dma_start(wdot_sb[0][:], wdot[:, 0:LOAD])
         nc.sync.dma_start(tfeat_sb[1][:], tfeat[:, LOAD : 2 * LOAD])
         nc.sync.dma_start(gain_col[:], ln_gain)
-        nc.sync.dma_start(bias_col[:], ln_bias)
-        nc.scalar.dma_start(wdot_sb[1][:], wdot[:, LOAD : 2 * LOAD])
         nc.sync.dma_start(w_lin_sb[:], w_lin)
+        nc.sync.dma_start(bias_col[:], ln_bias)
         nc.sync.dma_start(b_lin_col[:], b_lin)
         nc.sync.dma_start(offsets[:], offs)
         nc.sync.dma_start(window[:], base)
+        nc.sync.dma_start(wdot_sb[1][:], wdot[:, LOAD : 2 * LOAD])
 
         average = held.tile([P, P], F32, name="average")
         nc.vector.memset(average[:], 1.0 / P)
@@ -79,88 +81,82 @@ def tile_htr_kernel(tc, base, wdot, ln_gain, ln_bias, w_lin, b_lin, tfeat, w_t, 
         table_warmer = held.tile([P, 1], F32, name="table_warmer")
         nc.scalar.activation(table_warmer[:], eps_col[:], ACT.Silu)
 
-        gates = [held.tile([P, PIECE], F32, name=f"gate{piece}") for piece in range(N // PIECE)]
-        dws = [held.tile([P, PIECE], F32, name=f"dw{piece}") for piece in range(N // PIECE)]
-        centred, squared = {}, {}
-        banks_of_centred = ["norm_a", "norm_b"]
-        banks_of_var = ["norm_b", "norm_a"]
+        gates = [held.tile([P, PIECE], F32, name=f"gate{piece}") for piece in range(PIECES)]
+        dws = [held.tile([P, PIECE], F32, name=f"dw{piece}") for piece in range(PIECES)]
+        centred, squared, var_ps, normed = {}, {}, {}, {}
 
         def gate(c):
             act_feat = chunked.tile([P, CHUNK], BF16, name="act_feat")
             nc.scalar.activation(act_feat[:], chunk_of(tfeat_sb, c), ACT.Silu)
-            t_ps = psum.tile([P, CHUNK], F32, name="t_ps", tag="t_or_dw", bufs=2)
+            t_ps = psum.tile([P, CHUNK], F32, name="t_ps", tag="t_then_var")
             nc.tensor.matmul(t_ps[:], w_t_sb[:], act_feat[:], start=True, stop=True)
             nc.scalar.activation(chunk_in_piece(gates, c), t_ps[:], ACT.Silu, bias=b_t_col[:, 0:1])
 
         def centre_and_square(c, vector_is_free):
-            centred_ps = psum.tile([P, CHUNK], F32, name="centred_ps", tag=banks_of_centred[c // per_piece])
+            centred_ps = psum.tile([P, CHUNK], F32, name="centred_ps", bufs=4)
             nc.tensor.matmul(centred_ps[:], centre[:], chunk_of(wdot_sb, c), start=True, stop=True)
-            centred[c] = chunked.tile([P, CHUNK], F32, name="centred")
             squared[c] = chunked.tile([P, CHUNK], F32, name="squared")
             if vector_is_free:
+                centred[c] = chunked.tile([P, CHUNK], F32, name="centred_sb")
                 nc.vector.tensor_copy(centred[c][:], centred_ps[:])
                 nc.vector.tensor_tensor(squared[c][:], centred[c][:], centred_ps[:], ALU.mult)
             else:
+                centred[c] = centred_ps
                 nc.scalar.activation(squared[c][:], centred_ps[:], ACT.Square)
-                nc.scalar.activation(centred[c][:], centred_ps[:], ACT.Copy)
-
-        var_ps, dw_ps = {}, {}
 
         def mean_of_squares(c):
-            var_ps[c] = psum.tile([P, CHUNK], F32, name="var_ps", tag=banks_of_var[c // per_piece])
+            var_ps[c] = psum.tile([P, CHUNK], F32, name="var_ps", tag="t_then_var")
             nc.tensor.matmul(var_ps[c][:], average[:], squared[c][:], start=True, stop=True)
 
-        scaled = {}
-
-        def scale_by_root(c, multiplier):
+        def normalise(c):
             rstd = chunked.tile([P, CHUNK], F32, name="rstd")
             nc.scalar.activation(rstd[:], var_ps[c][:], ACT.Abs_reciprocal_sqrt, bias=eps_col[:, 0:1])
-            scaled[c] = chunked.tile([P, CHUNK], F32, name="scaled")
-            multiplier.tensor_tensor(scaled[c][:], centred[c][:], rstd[:], ALU.mult)
+            normed[c] = chunked.tile([P, CHUNK], BF16, name="normed")
+            nc.vector.scalar_tensor_tensor(normed[c][:], centred[c][:], gain_col[:, 0:1], rstd[:], ALU.mult, ALU.mult)
 
-        def linear(c, vector_is_free):
-            normed = chunked.tile([P, CHUNK], BF16, name="normed")
-            if vector_is_free:
-                nc.vector.tensor_scalar(normed[:], scaled[c][:], gain_col[:, 0:1], bias_col[:, 0:1], ALU.mult, ALU.add)
-            else:
-                nc.scalar.activation(normed[:], scaled[c][:], ACT.Identity, bias=bias_col[:, 0:1], scale=gain_col[:, 0:1])
-            dw_ps[c] = psum.tile([P, CHUNK], F32, name="dw_ps", tag="t_or_dw", bufs=2)
-            nc.tensor.matmul(dw_ps[c][:], w_lin_sb[:], normed[:], start=True, stop=True)
-
-        def add_b_lin(c):
-            nc.scalar.activation(chunk_in_piece(dws, c), dw_ps[c][:], ACT.Identity, bias=b_lin_col[:, 0:1])
+        def linear(c):
+            dw_ps = psum.tile([P, CHUNK], F32, name="dw_ps")
+            nc.tensor.matmul(dw_ps[:], w_lin_sb[:], normed[c][:], start=True, stop=True)
+            nc.scalar.activation(chunk_in_piece(dws, c), dw_ps[:], ACT.Identity, bias=both_biases[:, 0:1])
 
         def place(piece):
             piece_offsets = offsets[:, piece * (PIECE // 16) : (piece + 1) * (PIECE // 16)]
             nc.vector.tensor_tensor(window[:].indirect(piece_offsets), dws[piece][:], gates[piece][:], ALU.mult)
 
-        for c in first_piece:
+        for c in chunks_of(0):
             gate(c)
-        for c in first_piece:
+        for c in chunks_of(0):
             centre_and_square(c, True)
-        for c in second_piece:
+        for c in chunks_of(1):
             gate(c)
-        for c in first_piece:
+        for c in chunks_of(1):
+            centre_and_square(c, True)
+        for c in chunks_of(2):
+            gate(c)
+        for c in chunks_of(3):
+            gate(c)
+
+        w_lin_f32 = held.tile([P, P], F32, name="w_lin_f32")
+        nc.vector.tensor_copy(w_lin_f32[:], w_lin_sb[:])
+        bias_ps = psum.tile([P, 1], F32, name="bias_ps", tag="dw_ps")
+        nc.tensor.matmul(bias_ps[:], w_lin_f32[:], bias_col[:], start=True, stop=True)
+        both_biases = held.tile([P, 1], F32, name="both_biases")
+        nc.vector.tensor_tensor(both_biases[:], bias_ps[:], b_lin_col[:], ALU.add)
+
+        for c in chunks_of(0):
             mean_of_squares(c)
-        for c in first_piece:
-            scale_by_root(c, nc.vector)
-        for c in first_piece:
-            linear(c, True)
-        for c in first_piece:
-            add_b_lin(c)
-        place(0)
-        for round_no in range(per_piece + 3):
-            oldest = per_piece + round_no - 3
-            if oldest in second_piece:
-                add_b_lin(oldest)
-            if oldest + 1 in second_piece:
-                linear(oldest + 1, False)
-            if oldest + 2 in second_piece:
-                mean_of_squares(oldest + 2)
-                scale_by_root(oldest + 2, nc.gpsimd)
-            if oldest + 3 in second_piece:
-                centre_and_square(oldest + 3, False)
-        place(1)
+            normalise(c)
+        for piece in range(PIECES):
+            if piece + 2 < PIECES:
+                for c in chunks_of(piece + 2):
+                    centre_and_square(c, False)
+            if piece + 1 < PIECES:
+                for c in chunks_of(piece + 1):
+                    mean_of_squares(c)
+                    normalise(c)
+            for c in chunks_of(piece):
+                linear(c)
+            place(piece)
 
         nc.sync.dma_start(out[:, 0 : S // 2], window[:, 0 : S // 2])
         nc.scalar.dma_start(out[:, S // 2 : S], window[:, S // 2 : S])

@@ -9,37 +9,26 @@ ALU = mybir.AluOpType
 P = 128
 S = 4096
 N = 2048
-LOAD = 1024
-CHUNK = 256
 PIECE = 512
-CHUNKS = N // CHUNK
 PIECES = N // PIECE
+HALF = N // 2
 LN_EPS = 1e-5
 FLOPS = 2 * 2 * P * P * N
 
 
 def tile_htr_kernel(tc, base, wdot, ln_gain, ln_bias, w_lin, b_lin, tfeat, w_t, b_t, offs, out):
     nc = tc.nc
-    per_piece = PIECE // CHUNK
 
-    def chunks_of(piece):
-        return range(piece * per_piece, (piece + 1) * per_piece)
-
-    def chunk_of(loaded, c):
-        first = c * CHUNK
-        return loaded[first // LOAD][:, first % LOAD : first % LOAD + CHUNK]
-
-    def chunk_in_piece(factor, c):
-        first = (c % per_piece) * CHUNK
-        return factor[c // per_piece][:, first : first + CHUNK]
+    def piece_of(halves, piece):
+        first = piece * PIECE
+        return halves[first // HALF][:, first % HALF : first % HALF + PIECE]
 
     with (
         tc.tile_pool(name="held", bufs=1) as held,
-        tc.tile_pool(name="chunked", bufs=CHUNKS) as chunked,
         tc.psum_pool(name="psum", bufs=2) as psum,
     ):
-        tfeat_sb = [held.tile([P, LOAD], F32, name=f"tfeat_sb{i}") for i in range(N // LOAD)]
-        wdot_sb = [held.tile([P, LOAD], F32, name=f"wdot_sb{i}") for i in range(N // LOAD)]
+        tfeat_sb = [held.tile([P, HALF], F32, name=f"tfeat_sb{i}") for i in range(2)]
+        wdot_sb = [held.tile([P, HALF], F32, name=f"wdot_sb{i}") for i in range(2)]
         w_t_sb = held.tile([P, P], BF16, name="w_t_sb")
         w_lin_sb = held.tile([P, P], BF16, name="w_lin_sb")
         b_t_col = held.tile([P, 1], F32, name="b_t_col")
@@ -51,16 +40,16 @@ def tile_htr_kernel(tc, base, wdot, ln_gain, ln_bias, w_lin, b_lin, tfeat, w_t, 
 
         nc.sync.dma_start(w_t_sb[:], w_t)
         nc.sync.dma_start(b_t_col[:], b_t)
-        nc.sync.dma_start(tfeat_sb[0][:], tfeat[:, 0:LOAD])
-        nc.sync.dma_start(wdot_sb[0][:], wdot[:, 0:LOAD])
-        nc.sync.dma_start(tfeat_sb[1][:], tfeat[:, LOAD : 2 * LOAD])
-        nc.sync.dma_start(gain_col[:], ln_gain)
         nc.sync.dma_start(w_lin_sb[:], w_lin)
         nc.sync.dma_start(bias_col[:], ln_bias)
         nc.sync.dma_start(b_lin_col[:], b_lin)
+        nc.sync.dma_start(gain_col[:], ln_gain)
+        nc.sync.dma_start(wdot_sb[0][:], wdot[:, 0:HALF])
+        nc.sync.dma_start(tfeat_sb[0][:], tfeat[:, 0:HALF])
+        nc.sync.dma_start(tfeat_sb[1][:], tfeat[:, HALF:N])
+        nc.sync.dma_start(wdot_sb[1][:], wdot[:, HALF:N])
         nc.sync.dma_start(offsets[:], offs)
         nc.sync.dma_start(window[:], base)
-        nc.sync.dma_start(wdot_sb[1][:], wdot[:, LOAD : 2 * LOAD])
 
         average = held.tile([P, P], F32, name="average")
         nc.vector.memset(average[:], 1.0 / P)
@@ -83,79 +72,101 @@ def tile_htr_kernel(tc, base, wdot, ln_gain, ln_bias, w_lin, b_lin, tfeat, w_t, 
 
         gates = [held.tile([P, PIECE], F32, name=f"gate{piece}") for piece in range(PIECES)]
         dws = [held.tile([P, PIECE], F32, name=f"dw{piece}") for piece in range(PIECES)]
-        centred, squared, var_ps, normed = {}, {}, {}, {}
+        act_feat = [held.tile([P, HALF], BF16, name=f"act_feat{half}") for half in range(2)]
+        t_ps, centred_ps, centred, squared, var_ps, rstd, normed, dw_ps = {}, {}, {}, {}, {}, {}, {}, {}
 
-        def gate(c):
-            act_feat = chunked.tile([P, CHUNK], BF16, name="act_feat")
-            nc.scalar.activation(act_feat[:], chunk_of(tfeat_sb, c), ACT.Silu)
-            t_ps = psum.tile([P, CHUNK], F32, name="t_ps", tag="t_then_var")
-            nc.tensor.matmul(t_ps[:], w_t_sb[:], act_feat[:], start=True, stop=True)
-            nc.scalar.activation(chunk_in_piece(gates, c), t_ps[:], ACT.Silu, bias=b_t_col[:, 0:1])
+        def inner_silu(first, edges):
+            half, start = first // HALF, first % HALF
+            nc.scalar.activation(
+                act_feat[half][:, start : start + edges], tfeat_sb[half][:, start : start + edges], ACT.Silu
+            )
 
-        def centre_and_square(c, vector_is_free):
-            centred_ps = psum.tile([P, CHUNK], F32, name="centred_ps", bufs=4)
-            nc.tensor.matmul(centred_ps[:], centre[:], chunk_of(wdot_sb, c), start=True, stop=True)
-            squared[c] = chunked.tile([P, CHUNK], F32, name="squared")
-            if vector_is_free:
-                centred[c] = chunked.tile([P, CHUNK], F32, name="centred_sb")
-                nc.vector.tensor_copy(centred[c][:], centred_ps[:])
-                nc.vector.tensor_tensor(squared[c][:], centred[c][:], centred_ps[:], ALU.mult)
-            else:
-                centred[c] = centred_ps
-                nc.scalar.activation(squared[c][:], centred_ps[:], ACT.Square)
+        def gate_matmul(piece):
+            t_ps[piece] = psum.tile([P, PIECE], F32, name="t_ps", tag="t_then_dw", bufs=PIECES)
+            nc.tensor.matmul(t_ps[piece][:], w_t_sb[:], piece_of(act_feat, piece), start=True, stop=True)
 
-        def mean_of_squares(c):
-            var_ps[c] = psum.tile([P, CHUNK], F32, name="var_ps", tag="t_then_var")
-            nc.tensor.matmul(var_ps[c][:], average[:], squared[c][:], start=True, stop=True)
+        def gate(piece):
+            nc.scalar.activation(gates[piece][:], t_ps[piece][:], ACT.Silu, bias=b_t_col[:, 0:1])
 
-        def normalise(c):
-            rstd = chunked.tile([P, CHUNK], F32, name="rstd")
-            nc.scalar.activation(rstd[:], var_ps[c][:], ACT.Abs_reciprocal_sqrt, bias=eps_col[:, 0:1])
-            normed[c] = chunked.tile([P, CHUNK], BF16, name="normed")
-            nc.vector.scalar_tensor_tensor(normed[c][:], centred[c][:], gain_col[:, 0:1], rstd[:], ALU.mult, ALU.mult)
+        def centre_features(piece):
+            centred_ps[piece] = psum.tile([P, PIECE], F32, name="centred_ps")
+            nc.tensor.matmul(centred_ps[piece][:], centre[:], piece_of(wdot_sb, piece), start=True, stop=True)
 
-        def linear(c):
-            dw_ps = psum.tile([P, CHUNK], F32, name="dw_ps")
-            nc.tensor.matmul(dw_ps[:], w_lin_sb[:], normed[c][:], start=True, stop=True)
-            nc.scalar.activation(chunk_in_piece(dws, c), dw_ps[:], ACT.Identity, bias=both_biases[:, 0:1])
+        def square_on_vector(piece):
+            centred[piece] = held.tile([P, PIECE], F32, name=f"centred_sb{piece}")
+            squared[piece] = held.tile([P, PIECE], F32, name=f"squared{piece}")
+            nc.vector.tensor_copy(centred[piece][:], centred_ps[piece][:])
+            nc.vector.tensor_tensor(squared[piece][:], centred[piece][:], centred_ps[piece][:], ALU.mult)
+
+        def square_on_scalar(piece):
+            centred[piece] = centred_ps[piece]
+            squared[piece] = held.tile([P, PIECE], F32, name=f"squared{piece}")
+            nc.scalar.activation(squared[piece][:], centred_ps[piece][:], ACT.Square)
+
+        def mean_of_squares(piece):
+            var_ps[piece] = psum.tile([P, PIECE], F32, name="var_ps")
+            nc.tensor.matmul(var_ps[piece][:], average[:], squared[piece][:], start=True, stop=True)
+
+        def root(piece):
+            rstd[piece] = held.tile([P, PIECE], F32, name=f"rstd{piece}")
+            nc.scalar.activation(rstd[piece][:], var_ps[piece][:], ACT.Abs_reciprocal_sqrt, bias=eps_col[:, 0:1])
+
+        def normalise(piece):
+            normed[piece] = held.tile([P, PIECE], BF16, name=f"normed{piece}")
+            nc.vector.scalar_tensor_tensor(
+                normed[piece][:], centred[piece][:], gain_col[:, 0:1], rstd[piece][:], ALU.mult, ALU.mult
+            )
+
+        def linear(piece):
+            dw_ps[piece] = psum.tile([P, PIECE], F32, name="dw_ps", tag="t_then_dw", bufs=PIECES)
+            nc.tensor.matmul(dw_ps[piece][:], w_lin_sb[:], normed[piece][:], start=True, stop=True)
+
+        def add_biases(piece):
+            nc.scalar.activation(dws[piece][:], dw_ps[piece][:], ACT.Identity, bias=both_biases[:, 0:1])
 
         def place(piece):
             piece_offsets = offsets[:, piece * (PIECE // 16) : (piece + 1) * (PIECE // 16)]
             nc.vector.tensor_tensor(window[:].indirect(piece_offsets), dws[piece][:], gates[piece][:], ALU.mult)
 
-        for c in chunks_of(0):
-            gate(c)
-        for c in chunks_of(0):
-            centre_and_square(c, True)
-        for c in chunks_of(1):
-            gate(c)
-        for c in chunks_of(1):
-            centre_and_square(c, True)
-        for c in chunks_of(2):
-            gate(c)
-        for c in chunks_of(3):
-            gate(c)
-
         w_lin_f32 = held.tile([P, P], F32, name="w_lin_f32")
         nc.vector.tensor_copy(w_lin_f32[:], w_lin_sb[:])
-        bias_ps = psum.tile([P, 1], F32, name="bias_ps", tag="dw_ps")
+        bias_ps = psum.tile([P, 1], F32, name="bias_ps", tag="var_ps")
         nc.tensor.matmul(bias_ps[:], w_lin_f32[:], bias_col[:], start=True, stop=True)
         both_biases = held.tile([P, 1], F32, name="both_biases")
         nc.vector.tensor_tensor(both_biases[:], bias_ps[:], b_lin_col[:], ALU.add)
 
-        for c in chunks_of(0):
-            mean_of_squares(c)
-            normalise(c)
+        centre_features(0)
+        square_on_vector(0)
+        centre_features(1)
+        square_on_vector(1)
+        inner_silu(0, HALF)
+        gate_matmul(0)
+        gate_matmul(1)
+        inner_silu(HALF, HALF)
+        gate_matmul(2)
+        gate_matmul(3)
+        mean_of_squares(0)
+        mean_of_squares(1)
         for piece in range(PIECES):
-            if piece + 2 < PIECES:
-                for c in chunks_of(piece + 2):
-                    centre_and_square(c, False)
-            if piece + 1 < PIECES:
-                for c in chunks_of(piece + 1):
-                    mean_of_squares(c)
-                    normalise(c)
-            for c in chunks_of(piece):
-                linear(c)
+            gate(piece)
+        for piece in range(2):
+            root(piece)
+            normalise(piece)
+            linear(piece)
+            add_biases(piece)
+        for piece in range(2, PIECES):
+            centre_features(piece)
+            square_on_scalar(piece)
+        for piece in range(2, PIECES):
+            mean_of_squares(piece)
+        for piece in range(2, PIECES):
+            root(piece)
+            normalise(piece)
+        place(0)
+        for piece in range(2, PIECES):
+            linear(piece)
+            add_biases(piece)
+        for piece in range(1, PIECES):
             place(piece)
 
         nc.sync.dma_start(out[:, 0 : S // 2], window[:, 0 : S // 2])

@@ -55,17 +55,10 @@ def tile_htr_kernel(tc, base, wdot, ln_gain, ln_bias, w_lin, b_lin, tfeat, w_t, 
         nc.vector.memset(average[:], 1.0 / P)
         eps_col = held.tile([P, 1], F32, name="eps_col")
         nc.vector.memset(eps_col[:], LN_EPS)
+        row_minus_column = held.tile([P, P], F32, name="row_minus_column")
+        nc.gpsimd.iota(row_minus_column[:], pattern=[[-1, P]], base=0, channel_multiplier=1, allow_small_or_imprecise_dtypes=True)
         centre = held.tile([P, P], F32, name="centre")
-        nc.gpsimd.memset(centre[:], -1.0 / P)
-        nc.gpsimd.affine_select(
-            out=centre[:],
-            in_=centre[:],
-            compare_op=ALU.not_equal,
-            fill=1.0 - 1.0 / P,
-            base=0,
-            pattern=[[-1, P]],
-            channel_multiplier=1,
-        )
+        nc.vector.tensor_scalar(centre[:], row_minus_column[:], 0.0, 1.0 / P, ALU.is_equal, ALU.subtract)
 
         table_warmer = held.tile([P, 1], F32, name="table_warmer")
         nc.scalar.activation(table_warmer[:], eps_col[:], ACT.Silu)
@@ -81,8 +74,8 @@ def tile_htr_kernel(tc, base, wdot, ln_gain, ln_bias, w_lin, b_lin, tfeat, w_t, 
                 act_feat[half][:, start : start + edges], tfeat_sb[half][:, start : start + edges], ACT.Silu
             )
 
-        def gate_matmul(piece):
-            t_ps[piece] = psum.tile([P, PIECE], F32, name="t_ps", tag="t_then_dw", bufs=PIECES)
+        def gate_matmul(piece, tag, bufs):
+            t_ps[piece] = psum.tile([P, PIECE], F32, name="t_ps", tag=tag, bufs=bufs)
             nc.tensor.matmul(t_ps[piece][:], w_t_sb[:], piece_of(act_feat, piece), start=True, stop=True)
 
         def gate(piece):
@@ -140,14 +133,12 @@ def tile_htr_kernel(tc, base, wdot, ln_gain, ln_bias, w_lin, b_lin, tfeat, w_t, 
         centre_features(1)
         square_on_vector(1)
         inner_silu(0, HALF)
-        gate_matmul(0)
-        gate_matmul(1)
+        gate_matmul(0, "t_then_dw", PIECES)
+        gate_matmul(1, "t_then_dw", PIECES)
         inner_silu(HALF, HALF)
-        gate_matmul(2)
-        gate_matmul(3)
         mean_of_squares(0)
         mean_of_squares(1)
-        for piece in range(PIECES):
+        for piece in range(2):
             gate(piece)
         for piece in range(2):
             root(piece)
@@ -166,6 +157,10 @@ def tile_htr_kernel(tc, base, wdot, ln_gain, ln_bias, w_lin, b_lin, tfeat, w_t, 
         for piece in range(2, PIECES):
             linear(piece)
             add_biases(piece)
+        for piece in range(2, PIECES):
+            gate_matmul(piece, "var_ps", 2)
+        for piece in range(2, PIECES):
+            gate(piece)
         for piece in range(1, PIECES):
             place(piece)
 

@@ -11,7 +11,8 @@ S = 4096
 N = 2048
 PIECE = 512
 PIECES = N // PIECE
-HALF = N // 2
+HALF = PIECE // 2
+PAIR = 2 * PIECE
 LN_EPS = 1e-5
 FLOPS = 2 * 2 * P * P * N
 
@@ -19,16 +20,14 @@ FLOPS = 2 * 2 * P * P * N
 def tile_htr_kernel(tc, base, wdot, ln_gain, ln_bias, w_lin, b_lin, tfeat, w_t, b_t, offs, out):
     nc = tc.nc
 
-    def piece_of(halves, piece):
-        first = piece * PIECE
-        return halves[first // HALF][:, first % HALF : first % HALF + PIECE]
-
     with (
         tc.tile_pool(name="held", bufs=1) as held,
-        tc.psum_pool(name="psum", bufs=2) as psum,
+        tc.psum_pool(name="psum", bufs=1) as psum,
     ):
-        tfeat_sb = [held.tile([P, HALF], F32, name=f"tfeat_sb{i}") for i in range(2)]
-        wdot_sb = [held.tile([P, HALF], F32, name=f"wdot_sb{i}") for i in range(2)]
+        wdot_sb = [held.tile([P, PIECE], F32, name=f"wdot_sb{piece}") for piece in range(2)]
+        wdot_late = held.tile([P, PAIR], F32, name="wdot_late")
+        tfeat_early = held.tile([P, PAIR], F32, name="tfeat_early")
+        tfeat_late = held.tile([P, PAIR], F32, name="tfeat_late")
         w_t_sb = held.tile([P, P], BF16, name="w_t_sb")
         w_lin_sb = held.tile([P, P], BF16, name="w_lin_sb")
         b_t_col = held.tile([P, 1], F32, name="b_t_col")
@@ -38,131 +37,153 @@ def tile_htr_kernel(tc, base, wdot, ln_gain, ln_bias, w_lin, b_lin, tfeat, w_t, 
         offsets = held.tile([P, N // 16], U16, name="offsets")
         window = held.tile([P, S], F32, name="window")
 
+        nc.sync.dma_start(wdot_sb[0][:], wdot[:, 0:PIECE])
+        nc.sync.dma_start(tfeat_early[:], tfeat[:, 0:PAIR])
+        nc.sync.dma_start(tfeat_late[:], tfeat[:, PAIR:N])
         nc.sync.dma_start(w_t_sb[:], w_t)
         nc.sync.dma_start(b_t_col[:], b_t)
+        nc.sync.dma_start(wdot_sb[1][:], wdot[:, PIECE:PAIR])
         nc.sync.dma_start(w_lin_sb[:], w_lin)
+        nc.sync.dma_start(wdot_late[:], wdot[:, PAIR:N])
         nc.sync.dma_start(bias_col[:], ln_bias)
         nc.sync.dma_start(b_lin_col[:], b_lin)
         nc.sync.dma_start(gain_col[:], ln_gain)
-        nc.sync.dma_start(wdot_sb[0][:], wdot[:, 0:HALF])
-        nc.sync.dma_start(tfeat_sb[0][:], tfeat[:, 0:HALF])
-        nc.sync.dma_start(tfeat_sb[1][:], tfeat[:, HALF:N])
-        nc.sync.dma_start(wdot_sb[1][:], wdot[:, HALF:N])
         nc.sync.dma_start(offsets[:], offs)
         nc.sync.dma_start(window[:], base)
 
+        ones = held.tile([P, P], F32, name="ones")
+        nc.vector.memset(ones[:], 1.0)
+        column_number = held.tile([P, P], F32, name="column_number", align_bytes=64)
+        nc.vector.tensor_tensor_scan(column_number[:], ones[:], ones[:], -1.0, ALU.mult, ALU.add)
+        block_turned = held.tile([P, P], F32, name="block_turned", align_bytes=64)
+        nc.vector.transpose(block_turned[:], column_number[:])
+        centre = held.tile([P, P], F32, name="centre")
+        for first in range(0, P, 32):
+            rows = slice(first, first + 32)
+            nc.vector.tensor_scalar(
+                centre[rows, :], column_number[rows, :], block_turned[rows, first : first + 1], 1.0 / P,
+                ALU.is_equal, ALU.subtract,
+            )
         average = held.tile([P, P], F32, name="average")
         nc.vector.memset(average[:], 1.0 / P)
         eps_col = held.tile([P, 1], F32, name="eps_col")
+        eps_of_piece_2 = held.tile([P, 1], F32, name="eps_of_piece_2", tag="dw1")
         nc.vector.memset(eps_col[:], LN_EPS)
-        row_minus_column = held.tile([P, P], F32, name="row_minus_column")
-        nc.gpsimd.iota(row_minus_column[:], pattern=[[-1, P]], base=0, channel_multiplier=1, allow_small_or_imprecise_dtypes=True)
-        centre = held.tile([P, P], F32, name="centre")
-        nc.vector.tensor_scalar(centre[:], row_minus_column[:], 0.0, 1.0 / P, ALU.is_equal, ALU.subtract)
+        nc.vector.memset(eps_of_piece_2[:], LN_EPS)
 
         table_warmer = held.tile([P, 1], F32, name="table_warmer")
         nc.scalar.activation(table_warmer[:], eps_col[:], ACT.Silu)
 
         gates = [held.tile([P, PIECE], F32, name=f"gate{piece}") for piece in range(PIECES)]
         dws = [held.tile([P, PIECE], F32, name=f"dw{piece}") for piece in range(PIECES)]
-        act_feat = [held.tile([P, HALF], BF16, name=f"act_feat{half}") for half in range(2)]
-        t_ps, centred_ps, centred, squared, var_ps, rstd, normed, dw_ps = {}, {}, {}, {}, {}, {}, {}, {}
+        rstd = [held.tile([P, PIECE], F32, name=f"rstd{piece}") for piece in range(PIECES)]
+        normed = [held.tile([P, PIECE], BF16, name=f"normed{piece}") for piece in range(PIECES)]
+        act_feat_early = held.tile([P, PAIR], BF16, name="act_feat_early")
+        act_feat_late = held.tile([P, PAIR], BF16, name="act_feat_late")
+        squared_early = held.tile([P, PAIR], F32, name="squared_early")
+        squared_late = held.tile([P, PAIR], F32, name="squared_late", tag="normed0")
+        whole, first, second = slice(0, PIECE), slice(0, HALF), slice(HALF, PIECE)
 
-        def inner_silu(first, edges):
-            half, start = first // HALF, first % HALF
-            nc.scalar.activation(
-                act_feat[half][:, start : start + edges], tfeat_sb[half][:, start : start + edges], ACT.Silu
+        def part(pair, piece, columns=whole):
+            start = piece % 2 * PIECE
+            return pair[:, start + columns.start : start + columns.stop]
+
+        def bank(name):
+            return psum.tile([P, PIECE], F32, name=name)
+
+        def centre_features(centred_ps, piece, columns=whole):
+            source = wdot_sb[piece][:, columns] if piece < 2 else part(wdot_late, piece)
+            nc.tensor.matmul(centred_ps[:, columns], centre[:], source, start=True, stop=True)
+
+        def square_on_vector(centred_ps, piece, columns):
+            centred_sb = held.tile([P, PIECE], F32, name=f"centred_sb{piece}_{columns.start}")
+            nc.vector.tensor_copy(centred_sb[:, columns], centred_ps[:, columns])
+            nc.vector.tensor_tensor(
+                part(squared_early, piece, columns), centred_sb[:, columns], centred_ps[:, columns], ALU.mult
             )
 
-        def gate_matmul(piece, tag, bufs):
-            t_ps[piece] = psum.tile([P, PIECE], F32, name="t_ps", tag=tag, bufs=bufs)
-            nc.tensor.matmul(t_ps[piece][:], w_t_sb[:], piece_of(act_feat, piece), start=True, stop=True)
+        def square_on_scalar(centred_ps, piece):
+            nc.scalar.activation(part(squared_late, piece), centred_ps[:], ACT.Square)
 
-        def gate(piece):
-            nc.scalar.activation(gates[piece][:], t_ps[piece][:], ACT.Silu, bias=b_t_col[:, 0:1])
+        def mean_of_squares(var_ps, squared, piece, columns=whole):
+            nc.tensor.matmul(var_ps[:, columns], average[:], part(squared, piece, columns), start=True, stop=True)
 
-        def centre_features(piece):
-            centred_ps[piece] = psum.tile([P, PIECE], F32, name="centred_ps")
-            nc.tensor.matmul(centred_ps[piece][:], centre[:], piece_of(wdot_sb, piece), start=True, stop=True)
+        def root(var_ps, piece, columns=whole, eps=eps_col):
+            nc.scalar.activation(rstd[piece][:, columns], var_ps[:, columns], ACT.Abs_reciprocal_sqrt, bias=eps[:, 0:1])
 
-        def square_on_vector(piece):
-            centred[piece] = held.tile([P, PIECE], F32, name=f"centred_sb{piece}")
-            squared[piece] = held.tile([P, PIECE], F32, name=f"squared{piece}")
-            nc.vector.tensor_copy(centred[piece][:], centred_ps[piece][:])
-            nc.vector.tensor_tensor(squared[piece][:], centred[piece][:], centred_ps[piece][:], ALU.mult)
-
-        def square_on_scalar(piece):
-            centred[piece] = centred_ps[piece]
-            squared[piece] = held.tile([P, PIECE], F32, name=f"squared{piece}")
-            nc.scalar.activation(squared[piece][:], centred_ps[piece][:], ACT.Square)
-
-        def mean_of_squares(piece):
-            var_ps[piece] = psum.tile([P, PIECE], F32, name="var_ps")
-            nc.tensor.matmul(var_ps[piece][:], average[:], squared[piece][:], start=True, stop=True)
-
-        def root(piece):
-            rstd[piece] = held.tile([P, PIECE], F32, name=f"rstd{piece}")
-            nc.scalar.activation(rstd[piece][:], var_ps[piece][:], ACT.Abs_reciprocal_sqrt, bias=eps_col[:, 0:1])
-
-        def normalise(piece):
-            normed[piece] = held.tile([P, PIECE], BF16, name=f"normed{piece}")
+        def normalise(centred_ps, piece, columns=whole):
             nc.vector.scalar_tensor_tensor(
-                normed[piece][:], centred[piece][:], gain_col[:, 0:1], rstd[piece][:], ALU.mult, ALU.mult
+                normed[piece][:, columns], centred_ps[:, columns], gain_col[:, 0:1], rstd[piece][:, columns], ALU.mult, ALU.mult
             )
 
-        def linear(piece):
-            dw_ps[piece] = psum.tile([P, PIECE], F32, name="dw_ps", tag="t_then_dw", bufs=PIECES)
-            nc.tensor.matmul(dw_ps[piece][:], w_lin_sb[:], normed[piece][:], start=True, stop=True)
+        def linear(dw_ps, piece, columns=whole):
+            nc.tensor.matmul(dw_ps[:, columns], w_lin_sb[:], normed[piece][:, columns], start=True, stop=True)
+            nc.scalar.activation(dws[piece][:, columns], dw_ps[:, columns], ACT.Identity, bias=both_biases[:, 0:1])
 
-        def add_biases(piece):
-            nc.scalar.activation(dws[piece][:], dw_ps[piece][:], ACT.Identity, bias=both_biases[:, 0:1])
+        def gate(t_ps, act_feat, piece):
+            nc.tensor.matmul(t_ps[:], w_t_sb[:], part(act_feat, piece), start=True, stop=True)
+            nc.scalar.activation(gates[piece][:], t_ps[:], ACT.Silu, bias=b_t_col[:, 0:1])
 
         def place(piece):
             piece_offsets = offsets[:, piece * (PIECE // 16) : (piece + 1) * (PIECE // 16)]
             nc.vector.tensor_tensor(window[:].indirect(piece_offsets), dws[piece][:], gates[piece][:], ALU.mult)
 
+        first_centred_0, second_centred_0 = bank("even_a"), bank("odd_a")
+        centre_features(first_centred_0, 0, first)
+        centre_features(second_centred_0, 0, second)
+        nc.scalar.activation(act_feat_early[:], tfeat_early[:], ACT.Silu)
+        square_on_vector(first_centred_0, 0, first)
+        square_on_vector(second_centred_0, 0, second)
+        gate(bank("even_b"), act_feat_early, 0)
+        gate(bank("odd_b"), act_feat_early, 1)
+        nc.scalar.activation(act_feat_late[:], tfeat_late[:], ACT.Silu)
+        centred_1 = bank("extra_a")
+        centre_features(centred_1, 1)
+        square_on_vector(centred_1, 1, first)
+        square_on_vector(centred_1, 1, second)
+
         w_lin_f32 = held.tile([P, P], F32, name="w_lin_f32")
         nc.vector.tensor_copy(w_lin_f32[:], w_lin_sb[:])
-        bias_ps = psum.tile([P, 1], F32, name="bias_ps", tag="var_ps")
+        bias_ps = psum.tile([P, 1], F32, name="bias_ps")
         nc.tensor.matmul(bias_ps[:], w_lin_f32[:], bias_col[:], start=True, stop=True)
         both_biases = held.tile([P, 1], F32, name="both_biases")
         nc.vector.tensor_tensor(both_biases[:], bias_ps[:], b_lin_col[:], ALU.add)
 
-        centre_features(0)
-        square_on_vector(0)
-        centre_features(1)
-        square_on_vector(1)
-        inner_silu(0, HALF)
-        gate_matmul(0, "t_then_dw", PIECES)
-        gate_matmul(1, "t_then_dw", PIECES)
-        inner_silu(HALF, HALF)
-        mean_of_squares(0)
-        mean_of_squares(1)
-        for piece in range(2):
-            gate(piece)
-        for piece in range(2):
-            root(piece)
-            normalise(piece)
-            linear(piece)
-            add_biases(piece)
-        for piece in range(2, PIECES):
-            centre_features(piece)
-            square_on_scalar(piece)
-        for piece in range(2, PIECES):
-            mean_of_squares(piece)
-        for piece in range(2, PIECES):
-            root(piece)
-            normalise(piece)
+        var_0 = bank("even_b")
+        mean_of_squares(var_0, squared_early, 0, first)
+        mean_of_squares(var_0, squared_early, 0, second)
+        root(var_0, 0, first)
+        root(var_0, 0, second)
+        normalise(first_centred_0, 0, first)
+        normalise(second_centred_0, 0, second)
+        linear(bank("even_c"), 0, first)
+        linear(bank("odd_c"), 0, second)
+        var_1 = bank("odd_b")
+        mean_of_squares(var_1, squared_early, 1, first)
+        mean_of_squares(var_1, squared_early, 1, second)
+        root(var_1, 1)
+        normalise(centred_1, 1)
+        linear(bank("odd_c"), 1)
         place(0)
-        for piece in range(2, PIECES):
-            linear(piece)
-            add_biases(piece)
-        for piece in range(2, PIECES):
-            gate_matmul(piece, "var_ps", 2)
-        for piece in range(2, PIECES):
-            gate(piece)
-        for piece in range(1, PIECES):
-            place(piece)
+        centred_2, centred_3 = bank("even_a"), bank("odd_a")
+        centre_features(centred_2, 2)
+        centre_features(centred_3, 3)
+        square_on_scalar(centred_2, 2)
+        square_on_scalar(centred_3, 3)
+        var_2, var_3 = bank("even_c"), bank("odd_b")
+        mean_of_squares(var_2, squared_late, 2)
+        mean_of_squares(var_3, squared_late, 3)
+        root(var_2, 2, eps=eps_of_piece_2)
+        root(var_3, 3)
+        normalise(centred_2, 2)
+        place(1)
+        normalise(centred_3, 3)
+        linear(bank("even_c"), 2)
+        gate(bank("odd_b"), act_feat_late, 2)
+        place(2)
+        gate(bank("odd_b"), act_feat_late, 3)
+        linear(bank("even_c"), 3)
+        place(3)
 
         nc.sync.dma_start(out[:, 0 : S // 2], window[:, 0 : S // 2])
         nc.scalar.dma_start(out[:, S // 2 : S], window[:, S // 2 : S])

@@ -24,10 +24,10 @@ def tile_htr_kernel(tc, base, wdot, ln_gain, ln_bias, w_lin, b_lin, tfeat, w_t, 
         tc.tile_pool(name="held", bufs=1) as held,
         tc.psum_pool(name="psum", bufs=1) as psum,
     ):
-        wdot_sb = [held.tile([P, PIECE], F32, name=f"wdot_sb{piece}") for piece in range(2)]
+        wdot_halves = [held.tile([P, HALF], F32, name=f"wdot_half{half}") for half in range(2)]
+        wdot_sb = held.tile([P, PIECE], F32, name="wdot_sb")
         wdot_late = held.tile([P, PAIR], F32, name="wdot_late")
-        tfeat_early = held.tile([P, PAIR], F32, name="tfeat_early")
-        tfeat_late = held.tile([P, PAIR], F32, name="tfeat_late")
+        tfeat_sb = [held.tile([P, PIECE], F32, name=f"tfeat_sb{piece}") for piece in range(PIECES)]
         w_t_sb = held.tile([P, P], BF16, name="w_t_sb")
         w_lin_sb = held.tile([P, P], BF16, name="w_lin_sb")
         b_t_col = held.tile([P, 1], F32, name="b_t_col")
@@ -37,19 +37,24 @@ def tile_htr_kernel(tc, base, wdot, ln_gain, ln_bias, w_lin, b_lin, tfeat, w_t, 
         offsets = held.tile([P, N // 16], U16, name="offsets")
         window = held.tile([P, S], F32, name="window")
 
-        nc.sync.dma_start(wdot_sb[0][:], wdot[:, 0:PIECE])
-        nc.sync.dma_start(tfeat_early[:], tfeat[:, 0:PAIR])
-        nc.sync.dma_start(tfeat_late[:], tfeat[:, PAIR:N])
+        def load_tfeat(piece):
+            nc.sync.dma_start(tfeat_sb[piece][:], tfeat[:, piece * PIECE : (piece + 1) * PIECE])
+
+        nc.sync.dma_start(wdot_halves[0][:], wdot[:, 0:HALF])
+        nc.sync.dma_start(wdot_halves[1][:], wdot[:, HALF:PIECE])
         nc.sync.dma_start(w_t_sb[:], w_t)
+        for piece in range(3):
+            load_tfeat(piece)
         nc.sync.dma_start(b_t_col[:], b_t)
-        nc.sync.dma_start(wdot_sb[1][:], wdot[:, PIECE:PAIR])
+        nc.sync.dma_start(wdot_sb[:], wdot[:, PIECE:PAIR])
         nc.sync.dma_start(w_lin_sb[:], w_lin)
-        nc.sync.dma_start(wdot_late[:], wdot[:, PAIR:N])
         nc.sync.dma_start(bias_col[:], ln_bias)
+        nc.sync.dma_start(wdot_late[:], wdot[:, PAIR:N])
         nc.sync.dma_start(b_lin_col[:], b_lin)
         nc.sync.dma_start(gain_col[:], ln_gain)
         nc.sync.dma_start(offsets[:], offs)
         nc.sync.dma_start(window[:], base)
+        load_tfeat(3)
 
         ones = held.tile([P, P], F32, name="ones")
         nc.vector.memset(ones[:], 1.0)
@@ -66,21 +71,24 @@ def tile_htr_kernel(tc, base, wdot, ln_gain, ln_bias, w_lin, b_lin, tfeat, w_t, 
             )
         average = held.tile([P, P], F32, name="average")
         nc.vector.memset(average[:], 1.0 / P)
-        eps_col = held.tile([P, 1], F32, name="eps_col")
-        eps_of_piece_2 = held.tile([P, 1], F32, name="eps_of_piece_2", tag="dw1")
-        nc.vector.memset(eps_col[:], LN_EPS)
-        nc.vector.memset(eps_of_piece_2[:], LN_EPS)
+        eps_tags = ["eps0", "eps1", "dw1", "act_feat3"]
+        eps_cols = [held.tile([P, 1], F32, name=f"eps{piece}", tag=eps_tags[piece]) for piece in range(PIECES)]
+        for eps_col in eps_cols:
+            nc.vector.memset(eps_col[:], LN_EPS)
 
         table_warmer = held.tile([P, 1], F32, name="table_warmer")
-        nc.scalar.activation(table_warmer[:], eps_col[:], ACT.Silu)
+        nc.scalar.activation(table_warmer[:], eps_cols[0][:], ACT.Silu)
 
         gates = [held.tile([P, PIECE], F32, name=f"gate{piece}") for piece in range(PIECES)]
         dws = [held.tile([P, PIECE], F32, name=f"dw{piece}") for piece in range(PIECES)]
         rstd = [held.tile([P, PIECE], F32, name=f"rstd{piece}") for piece in range(PIECES)]
-        normed = [held.tile([P, PIECE], BF16, name=f"normed{piece}") for piece in range(PIECES)]
-        act_feat_early = held.tile([P, PAIR], BF16, name="act_feat_early")
-        act_feat_late = held.tile([P, PAIR], BF16, name="act_feat_late")
+        normed = [
+            held.tile([P, PIECE], BF16, name=f"normed{piece}", tag="dw0" if piece == 2 else f"normed{piece}")
+            for piece in range(PIECES)
+        ]
+        act_feat = [held.tile([P, PIECE], BF16, name=f"act_feat{piece}") for piece in range(PIECES)]
         squared_early = held.tile([P, PAIR], F32, name="squared_early")
+        centred_sb = held.tile([P, PAIR], F32, name="centred_sb")
         squared_late = held.tile([P, PAIR], F32, name="squared_late", tag="normed0")
         whole, first, second = slice(0, PIECE), slice(0, HALF), slice(HALF, PIECE)
 
@@ -91,15 +99,15 @@ def tile_htr_kernel(tc, base, wdot, ln_gain, ln_bias, w_lin, b_lin, tfeat, w_t, 
         def bank(name):
             return psum.tile([P, PIECE], F32, name=name)
 
-        def centre_features(centred_ps, piece, columns=whole):
-            source = wdot_sb[piece][:, columns] if piece < 2 else part(wdot_late, piece)
+        def centre_features(centred_ps, source, columns=whole):
             nc.tensor.matmul(centred_ps[:, columns], centre[:], source, start=True, stop=True)
 
+        def copy_to_sbuf(centred_ps, piece, columns):
+            nc.vector.tensor_copy(part(centred_sb, piece, columns), centred_ps[:, columns])
+
         def square_on_vector(centred_ps, piece, columns):
-            centred_sb = held.tile([P, PIECE], F32, name=f"centred_sb{piece}_{columns.start}")
-            nc.vector.tensor_copy(centred_sb[:, columns], centred_ps[:, columns])
             nc.vector.tensor_tensor(
-                part(squared_early, piece, columns), centred_sb[:, columns], centred_ps[:, columns], ALU.mult
+                part(squared_early, piece, columns), part(centred_sb, piece, columns), centred_ps[:, columns], ALU.mult
             )
 
         def square_on_scalar(centred_ps, piece):
@@ -108,20 +116,23 @@ def tile_htr_kernel(tc, base, wdot, ln_gain, ln_bias, w_lin, b_lin, tfeat, w_t, 
         def mean_of_squares(var_ps, squared, piece, columns=whole):
             nc.tensor.matmul(var_ps[:, columns], average[:], part(squared, piece, columns), start=True, stop=True)
 
-        def root(var_ps, piece, columns=whole, eps=eps_col):
-            nc.scalar.activation(rstd[piece][:, columns], var_ps[:, columns], ACT.Abs_reciprocal_sqrt, bias=eps[:, 0:1])
+        def root(var_ps, piece, columns=whole):
+            nc.scalar.activation(rstd[piece][:, columns], var_ps[:, columns], ACT.Abs_reciprocal_sqrt, bias=eps_cols[piece][:, 0:1])
 
-        def normalise(centred_ps, piece, columns=whole):
+        def normalise(centred, piece, columns=whole):
             nc.vector.scalar_tensor_tensor(
-                normed[piece][:, columns], centred_ps[:, columns], gain_col[:, 0:1], rstd[piece][:, columns], ALU.mult, ALU.mult
+                normed[piece][:, columns], centred, gain_col[:, 0:1], rstd[piece][:, columns], ALU.mult, ALU.mult
             )
 
         def linear(dw_ps, piece, columns=whole):
             nc.tensor.matmul(dw_ps[:, columns], w_lin_sb[:], normed[piece][:, columns], start=True, stop=True)
             nc.scalar.activation(dws[piece][:, columns], dw_ps[:, columns], ACT.Identity, bias=both_biases[:, 0:1])
 
-        def gate(t_ps, act_feat, piece):
-            nc.tensor.matmul(t_ps[:], w_t_sb[:], part(act_feat, piece), start=True, stop=True)
+        def inner_silu(piece):
+            nc.scalar.activation(act_feat[piece][:], tfeat_sb[piece][:], ACT.Silu)
+
+        def gate(t_ps, piece):
+            nc.tensor.matmul(t_ps[:], w_t_sb[:], act_feat[piece][:], start=True, stop=True)
             nc.scalar.activation(gates[piece][:], t_ps[:], ACT.Silu, bias=b_t_col[:, 0:1])
 
         def place(piece):
@@ -129,16 +140,20 @@ def tile_htr_kernel(tc, base, wdot, ln_gain, ln_bias, w_lin, b_lin, tfeat, w_t, 
             nc.vector.tensor_tensor(window[:].indirect(piece_offsets), dws[piece][:], gates[piece][:], ALU.mult)
 
         first_centred_0, second_centred_0 = bank("even_a"), bank("odd_a")
-        centre_features(first_centred_0, 0, first)
-        centre_features(second_centred_0, 0, second)
-        nc.scalar.activation(act_feat_early[:], tfeat_early[:], ACT.Silu)
+        centre_features(first_centred_0, wdot_halves[0][:], first)
+        centre_features(second_centred_0, wdot_halves[1][:], second)
+        for piece in range(3):
+            inner_silu(piece)
+        copy_to_sbuf(first_centred_0, 0, first)
+        copy_to_sbuf(second_centred_0, 0, second)
         square_on_vector(first_centred_0, 0, first)
         square_on_vector(second_centred_0, 0, second)
-        gate(bank("even_b"), act_feat_early, 0)
-        gate(bank("odd_b"), act_feat_early, 1)
-        nc.scalar.activation(act_feat_late[:], tfeat_late[:], ACT.Silu)
+        gate(bank("even_b"), 0)
+        gate(bank("odd_b"), 1)
         centred_1 = bank("extra_a")
-        centre_features(centred_1, 1)
+        centre_features(centred_1, wdot_sb[:])
+        copy_to_sbuf(centred_1, 1, first)
+        copy_to_sbuf(centred_1, 1, second)
         square_on_vector(centred_1, 1, first)
         square_on_vector(centred_1, 1, second)
 
@@ -149,40 +164,41 @@ def tile_htr_kernel(tc, base, wdot, ln_gain, ln_bias, w_lin, b_lin, tfeat, w_t, 
         both_biases = held.tile([P, 1], F32, name="both_biases")
         nc.vector.tensor_tensor(both_biases[:], bias_ps[:], b_lin_col[:], ALU.add)
 
-        var_0 = bank("even_b")
+        var_0 = bank("odd_b")
         mean_of_squares(var_0, squared_early, 0, first)
         mean_of_squares(var_0, squared_early, 0, second)
         root(var_0, 0, first)
         root(var_0, 0, second)
-        normalise(first_centred_0, 0, first)
-        normalise(second_centred_0, 0, second)
+        normalise(first_centred_0[:, first], 0, first)
+        normalise(second_centred_0[:, second], 0, second)
         linear(bank("even_c"), 0, first)
         linear(bank("odd_c"), 0, second)
-        var_1 = bank("odd_b")
+        var_1 = bank("even_b")
         mean_of_squares(var_1, squared_early, 1, first)
         mean_of_squares(var_1, squared_early, 1, second)
         root(var_1, 1)
-        normalise(centred_1, 1)
-        linear(bank("odd_c"), 1)
+        normalise(centred_1[:], 1)
+        linear(bank("even_c"), 1)
         place(0)
-        centred_2, centred_3 = bank("even_a"), bank("odd_a")
-        centre_features(centred_2, 2)
-        centre_features(centred_3, 3)
+        centred_2, centred_3 = bank("odd_a"), bank("extra_a")
+        centre_features(centred_2, part(wdot_late, 2))
+        centre_features(centred_3, part(wdot_late, 3))
         square_on_scalar(centred_2, 2)
         square_on_scalar(centred_3, 3)
-        var_2, var_3 = bank("even_c"), bank("odd_b")
+        var_2, var_3 = bank("even_a"), bank("even_b")
         mean_of_squares(var_2, squared_late, 2)
         mean_of_squares(var_3, squared_late, 3)
-        root(var_2, 2, eps=eps_of_piece_2)
+        root(var_2, 2)
         root(var_3, 3)
-        normalise(centred_2, 2)
+        normalise(centred_2[:], 2)
         place(1)
-        normalise(centred_3, 3)
-        linear(bank("even_c"), 2)
-        gate(bank("odd_b"), act_feat_late, 2)
+        normalise(centred_3[:], 3)
+        linear(bank("even_a"), 2)
+        gate(bank("even_b"), 2)
         place(2)
-        gate(bank("odd_b"), act_feat_late, 3)
-        linear(bank("even_c"), 3)
+        inner_silu(3)
+        gate(bank("even_b"), 3)
+        linear(bank("even_a"), 3)
         place(3)
 
         nc.sync.dma_start(out[:, 0 : S // 2], window[:, 0 : S // 2])

@@ -24,10 +24,11 @@ def tile_htr_kernel(tc, base, wdot, ln_gain, ln_bias, w_lin, b_lin, tfeat, w_t, 
         tc.tile_pool(name="held", bufs=1) as held,
         tc.psum_pool(name="psum", bufs=1) as psum,
     ):
-        wdot_halves = [held.tile([P, HALF], F32, name=f"wdot_half{half}") for half in range(2)]
-        wdot_sb = held.tile([P, PIECE], F32, name="wdot_sb")
+        wdot_0 = held.tile([P, PIECE], F32, name="wdot_0")
+        wdot_1 = held.tile([P, PIECE], F32, name="wdot_1")
         wdot_late = held.tile([P, PAIR], F32, name="wdot_late")
-        tfeat_sb = [held.tile([P, PIECE], F32, name=f"tfeat_sb{piece}") for piece in range(PIECES)]
+        tfeat_early = held.tile([P, PAIR], F32, name="tfeat_early")
+        tfeat_late = held.tile([P, PAIR], F32, name="tfeat_late")
         w_t_sb = held.tile([P, P], BF16, name="w_t_sb")
         w_lin_sb = held.tile([P, P], BF16, name="w_lin_sb")
         b_t_col = held.tile([P, 1], F32, name="b_t_col")
@@ -37,24 +38,19 @@ def tile_htr_kernel(tc, base, wdot, ln_gain, ln_bias, w_lin, b_lin, tfeat, w_t, 
         offsets = held.tile([P, N // 16], U16, name="offsets")
         window = held.tile([P, S], F32, name="window")
 
-        def load_tfeat(piece):
-            nc.sync.dma_start(tfeat_sb[piece][:], tfeat[:, piece * PIECE : (piece + 1) * PIECE])
-
-        nc.sync.dma_start(wdot_halves[0][:], wdot[:, 0:HALF])
-        nc.sync.dma_start(wdot_halves[1][:], wdot[:, HALF:PIECE])
+        nc.sync.dma_start(wdot_0[:], wdot[:, 0:PIECE])
+        nc.sync.dma_start(tfeat_early[:], tfeat[:, 0:PAIR])
+        nc.sync.dma_start(tfeat_late[:], tfeat[:, PAIR:N])
         nc.sync.dma_start(w_t_sb[:], w_t)
-        for piece in range(3):
-            load_tfeat(piece)
         nc.sync.dma_start(b_t_col[:], b_t)
-        nc.sync.dma_start(wdot_sb[:], wdot[:, PIECE:PAIR])
+        nc.sync.dma_start(wdot_1[:], wdot[:, PIECE:PAIR])
         nc.sync.dma_start(w_lin_sb[:], w_lin)
         nc.sync.dma_start(bias_col[:], ln_bias)
-        nc.sync.dma_start(wdot_late[:], wdot[:, PAIR:N])
         nc.sync.dma_start(b_lin_col[:], b_lin)
+        nc.sync.dma_start(wdot_late[:], wdot[:, PAIR:N])
         nc.sync.dma_start(gain_col[:], ln_gain)
         nc.sync.dma_start(offsets[:], offs)
         nc.sync.dma_start(window[:], base)
-        load_tfeat(3)
 
         ones = held.tile([P, P], F32, name="ones")
         nc.vector.memset(ones[:], 1.0)
@@ -71,7 +67,7 @@ def tile_htr_kernel(tc, base, wdot, ln_gain, ln_bias, w_lin, b_lin, tfeat, w_t, 
             )
         average = held.tile([P, P], F32, name="average")
         nc.vector.memset(average[:], 1.0 / P)
-        eps_tags = ["eps0", "eps1", "dw1", "act_feat3"]
+        eps_tags = ["eps0", "eps1", "dw1", "gate2"]
         eps_cols = [held.tile([P, 1], F32, name=f"eps{piece}", tag=eps_tags[piece]) for piece in range(PIECES)]
         for eps_col in eps_cols:
             nc.vector.memset(eps_col[:], LN_EPS)
@@ -86,7 +82,8 @@ def tile_htr_kernel(tc, base, wdot, ln_gain, ln_bias, w_lin, b_lin, tfeat, w_t, 
             held.tile([P, PIECE], BF16, name=f"normed{piece}", tag="dw0" if piece == 2 else f"normed{piece}")
             for piece in range(PIECES)
         ]
-        act_feat = [held.tile([P, PIECE], BF16, name=f"act_feat{piece}") for piece in range(PIECES)]
+        act_feat_early = held.tile([P, PAIR], BF16, name="act_feat_early")
+        act_feat_late = held.tile([P, PAIR], BF16, name="act_feat_late")
         squared_early = held.tile([P, PAIR], F32, name="squared_early")
         centred_sb = held.tile([P, PAIR], F32, name="centred_sb")
         squared_late = held.tile([P, PAIR], F32, name="squared_late", tag="normed0")
@@ -110,8 +107,8 @@ def tile_htr_kernel(tc, base, wdot, ln_gain, ln_bias, w_lin, b_lin, tfeat, w_t, 
                 part(squared_early, piece, columns), part(centred_sb, piece, columns), centred_ps[:, columns], ALU.mult
             )
 
-        def square_on_scalar(centred_ps, piece):
-            nc.scalar.activation(part(squared_late, piece), centred_ps[:], ACT.Square)
+        def square_on_scalar(centred_ps, piece, columns=whole):
+            nc.scalar.activation(part(squared_late, piece, columns), centred_ps[:, columns], ACT.Square)
 
         def mean_of_squares(var_ps, squared, piece, columns=whole):
             nc.tensor.matmul(var_ps[:, columns], average[:], part(squared, piece, columns), start=True, stop=True)
@@ -128,77 +125,78 @@ def tile_htr_kernel(tc, base, wdot, ln_gain, ln_bias, w_lin, b_lin, tfeat, w_t, 
             nc.tensor.matmul(dw_ps[:, columns], w_lin_sb[:], normed[piece][:, columns], start=True, stop=True)
             nc.scalar.activation(dws[piece][:, columns], dw_ps[:, columns], ACT.Identity, bias=both_biases[:, 0:1])
 
-        def inner_silu(piece):
-            nc.scalar.activation(act_feat[piece][:], tfeat_sb[piece][:], ACT.Silu)
-
-        def gate(t_ps, piece):
-            nc.tensor.matmul(t_ps[:], w_t_sb[:], act_feat[piece][:], start=True, stop=True)
+        def gate(t_ps, act_feat, piece):
+            nc.tensor.matmul(t_ps[:], w_t_sb[:], part(act_feat, piece), start=True, stop=True)
             nc.scalar.activation(gates[piece][:], t_ps[:], ACT.Silu, bias=b_t_col[:, 0:1])
 
         def place(piece):
             piece_offsets = offsets[:, piece * (PIECE // 16) : (piece + 1) * (PIECE // 16)]
             nc.vector.tensor_tensor(window[:].indirect(piece_offsets), dws[piece][:], gates[piece][:], ALU.mult)
 
-        first_centred_0, second_centred_0 = bank("even_a"), bank("odd_a")
-        centre_features(first_centred_0, wdot_halves[0][:], first)
-        centre_features(second_centred_0, wdot_halves[1][:], second)
-        for piece in range(3):
-            inner_silu(piece)
+        first_centred_0, second_centred_0 = bank("first_a"), bank("second_a")
+        centre_features(first_centred_0, wdot_0[:, first], first)
+        centre_features(second_centred_0, wdot_0[:, second], second)
+        nc.scalar.activation(act_feat_early[:], tfeat_early[:], ACT.Silu)
+        nc.scalar.activation(act_feat_late[:], tfeat_late[:], ACT.Silu)
         copy_to_sbuf(first_centred_0, 0, first)
         copy_to_sbuf(second_centred_0, 0, second)
         square_on_vector(first_centred_0, 0, first)
         square_on_vector(second_centred_0, 0, second)
-        gate(bank("even_b"), 0)
-        gate(bank("odd_b"), 1)
-        centred_1 = bank("extra_a")
-        centre_features(centred_1, wdot_sb[:])
-        copy_to_sbuf(centred_1, 1, first)
-        copy_to_sbuf(centred_1, 1, second)
-        square_on_vector(centred_1, 1, first)
-        square_on_vector(centred_1, 1, second)
+        gate(bank("first_c"), act_feat_early, 0)
+        gate(bank("second_c"), act_feat_early, 1)
+        first_centred_1, second_centred_1 = bank("first_b"), bank("second_b")
+        centre_features(first_centred_1, wdot_1[:, first], first)
+        centre_features(second_centred_1, wdot_1[:, second], second)
+        copy_to_sbuf(first_centred_1, 1, first)
+        copy_to_sbuf(second_centred_1, 1, second)
+        square_on_vector(first_centred_1, 1, first)
+        square_on_vector(second_centred_1, 1, second)
 
         w_lin_f32 = held.tile([P, P], F32, name="w_lin_f32")
         nc.vector.tensor_copy(w_lin_f32[:], w_lin_sb[:])
-        bias_ps = psum.tile([P, 1], F32, name="bias_ps")
-        nc.tensor.matmul(bias_ps[:], w_lin_f32[:], bias_col[:], start=True, stop=True)
+        bias_ps = bank("second_d")
+        nc.tensor.matmul(bias_ps[:, 0:1], w_lin_f32[:], bias_col[:], start=True, stop=True)
         both_biases = held.tile([P, 1], F32, name="both_biases")
-        nc.vector.tensor_tensor(both_biases[:], bias_ps[:], b_lin_col[:], ALU.add)
+        nc.vector.tensor_tensor(both_biases[:], bias_ps[:, 0:1], b_lin_col[:], ALU.add)
 
-        var_0 = bank("odd_b")
+        var_0 = bank("second_c")
         mean_of_squares(var_0, squared_early, 0, first)
         mean_of_squares(var_0, squared_early, 0, second)
         root(var_0, 0, first)
         root(var_0, 0, second)
         normalise(first_centred_0[:, first], 0, first)
         normalise(second_centred_0[:, second], 0, second)
-        linear(bank("even_c"), 0, first)
-        linear(bank("odd_c"), 0, second)
-        var_1 = bank("even_b")
+        linear(bank("first_d"), 0, first)
+        linear(bank("second_d"), 0, second)
+        var_1 = bank("first_c")
         mean_of_squares(var_1, squared_early, 1, first)
         mean_of_squares(var_1, squared_early, 1, second)
         root(var_1, 1)
-        normalise(centred_1[:], 1)
-        linear(bank("even_c"), 1)
+        normalise(first_centred_1[:, first], 1, first)
+        normalise(part(centred_sb, 1, second), 1, second)
+        linear(bank("first_d"), 1)
         place(0)
-        centred_2, centred_3 = bank("odd_a"), bank("extra_a")
-        centre_features(centred_2, part(wdot_late, 2))
+        first_centred_2, second_centred_2, centred_3 = bank("second_b"), bank("second_a"), bank("first_b")
+        centre_features(first_centred_2, part(wdot_late, 2, first), first)
+        centre_features(second_centred_2, part(wdot_late, 2, second), second)
         centre_features(centred_3, part(wdot_late, 3))
-        square_on_scalar(centred_2, 2)
+        square_on_scalar(first_centred_2, 2, first)
+        square_on_scalar(second_centred_2, 2, second)
         square_on_scalar(centred_3, 3)
-        var_2, var_3 = bank("even_a"), bank("even_b")
+        var_2, var_3 = bank("first_a"), bank("first_c")
         mean_of_squares(var_2, squared_late, 2)
         mean_of_squares(var_3, squared_late, 3)
         root(var_2, 2)
         root(var_3, 3)
-        normalise(centred_2[:], 2)
+        normalise(first_centred_2[:, first], 2, first)
+        normalise(second_centred_2[:, second], 2, second)
         place(1)
         normalise(centred_3[:], 3)
-        linear(bank("even_a"), 2)
-        gate(bank("even_b"), 2)
+        linear(bank("first_a"), 2)
+        gate(bank("second_c"), act_feat_late, 2)
         place(2)
-        inner_silu(3)
-        gate(bank("even_b"), 3)
-        linear(bank("even_a"), 3)
+        gate(bank("second_c"), act_feat_late, 3)
+        linear(bank("first_a"), 3)
         place(3)
 
         nc.sync.dma_start(out[:, 0 : S // 2], window[:, 0 : S // 2])

@@ -199,5 +199,4 @@ def tile_htr_kernel(tc, base, wdot, ln_gain, ln_bias, w_lin, b_lin, tfeat, w_t, 
         linear(bank("first_a"), 3)
         place(3)
 
-        nc.sync.dma_start(out[:, 0 : S // 2], window[:, 0 : S // 2])
-        nc.scalar.dma_start(out[:, S // 2 : S], window[:, S // 2 : S])
+        nc.sync.dma_start(out, window[:])

import concourse.mybir as mybir

F32 = mybir.dt.float32
BF16 = mybir.dt.bfloat16
U16 = mybir.dt.uint16
ACT = mybir.ActivationFunctionType
ALU = mybir.AluOpType

P = 128
S = 4096
N = 2048
PIECE = 512
PIECES = N // PIECE
HALF = PIECE // 2
PAIR = 2 * PIECE
LN_EPS = 1e-5
FLOPS = 2 * 2 * P * P * N


def tile_htr_kernel(tc, base, wdot, ln_gain, ln_bias, w_lin, b_lin, tfeat, w_t, b_t, offs, out):
    nc = tc.nc

    with (
        tc.tile_pool(name="held", bufs=1) as held,
        tc.psum_pool(name="psum", bufs=1) as psum,
    ):
        wdot_0 = held.tile([P, PIECE], F32, name="wdot_0")
        wdot_1 = held.tile([P, PIECE], F32, name="wdot_1")
        wdot_late = held.tile([P, PAIR], F32, name="wdot_late")
        tfeat_early = held.tile([P, PAIR], F32, name="tfeat_early")
        tfeat_late = held.tile([P, PAIR], F32, name="tfeat_late")
        w_t_sb = held.tile([P, P], BF16, name="w_t_sb")
        w_lin_sb = held.tile([P, P], BF16, name="w_lin_sb")
        b_t_col = held.tile([P, 1], F32, name="b_t_col")
        gain_col = held.tile([P, 1], F32, name="gain_col")
        bias_col = held.tile([P, 1], F32, name="bias_col")
        b_lin_col = held.tile([P, 1], F32, name="b_lin_col")
        offsets = held.tile([P, N // 16], U16, name="offsets")
        window = held.tile([P, S], F32, name="window")

        nc.sync.dma_start(wdot_0[:], wdot[:, 0:PIECE])
        nc.sync.dma_start(tfeat_early[:], tfeat[:, 0:PAIR])
        nc.sync.dma_start(tfeat_late[:], tfeat[:, PAIR:N])
        nc.sync.dma_start(w_t_sb[:], w_t)
        nc.sync.dma_start(b_t_col[:], b_t)
        nc.sync.dma_start(wdot_1[:], wdot[:, PIECE:PAIR])
        nc.sync.dma_start(w_lin_sb[:], w_lin)
        nc.sync.dma_start(bias_col[:], ln_bias)
        nc.sync.dma_start(b_lin_col[:], b_lin)
        nc.sync.dma_start(wdot_late[:], wdot[:, PAIR:N])
        nc.sync.dma_start(gain_col[:], ln_gain)
        nc.sync.dma_start(offsets[:], offs)
        nc.sync.dma_start(window[:], base)

        ones = held.tile([P, P], F32, name="ones")
        nc.vector.memset(ones[:], 1.0)
        column_number = held.tile([P, P], F32, name="column_number", align_bytes=64)
        nc.vector.tensor_tensor_scan(column_number[:], ones[:], ones[:], -1.0, ALU.mult, ALU.add)
        block_turned = held.tile([P, P], F32, name="block_turned", align_bytes=64)
        nc.vector.transpose(block_turned[:], column_number[:])
        centre = held.tile([P, P], F32, name="centre")
        for first in range(0, P, 32):
            rows = slice(first, first + 32)
            nc.vector.tensor_scalar(
                centre[rows, :], column_number[rows, :], block_turned[rows, first : first + 1], 1.0 / P,
                ALU.is_equal, ALU.subtract,
            )
        average = held.tile([P, P], F32, name="average")
        nc.vector.memset(average[:], 1.0 / P)
        eps_tags = ["eps0", "eps1", "dw1", "gate2"]
        eps_cols = [held.tile([P, 1], F32, name=f"eps{piece}", tag=eps_tags[piece]) for piece in range(PIECES)]
        for eps_col in eps_cols:
            nc.vector.memset(eps_col[:], LN_EPS)

        table_warmer = held.tile([P, 1], F32, name="table_warmer")
        nc.scalar.activation(table_warmer[:], eps_cols[0][:], ACT.Silu)

        gates = [held.tile([P, PIECE], F32, name=f"gate{piece}") for piece in range(PIECES)]
        dws = [held.tile([P, PIECE], F32, name=f"dw{piece}") for piece in range(PIECES)]
        rstd = [held.tile([P, PIECE], F32, name=f"rstd{piece}") for piece in range(PIECES)]
        normed = [
            held.tile([P, PIECE], BF16, name=f"normed{piece}", tag="dw0" if piece == 2 else f"normed{piece}")
            for piece in range(PIECES)
        ]
        act_feat_early = held.tile([P, PAIR], BF16, name="act_feat_early")
        act_feat_late = held.tile([P, PAIR], BF16, name="act_feat_late")
        squared_early = held.tile([P, PAIR], F32, name="squared_early")
        centred_sb = held.tile([P, PAIR], F32, name="centred_sb")
        squared_late = held.tile([P, PAIR], F32, name="squared_late", tag="normed0")
        whole, first, second = slice(0, PIECE), slice(0, HALF), slice(HALF, PIECE)

        def part(pair, piece, columns=whole):
            start = piece % 2 * PIECE
            return pair[:, start + columns.start : start + columns.stop]

        def bank(name):
            return psum.tile([P, PIECE], F32, name=name)

        def centre_features(centred_ps, source, columns=whole):
            nc.tensor.matmul(centred_ps[:, columns], centre[:], source, start=True, stop=True)

        def copy_to_sbuf(centred_ps, piece, columns):
            nc.vector.tensor_copy(part(centred_sb, piece, columns), centred_ps[:, columns])

        def square_on_vector(centred_ps, piece, columns):
            nc.vector.tensor_tensor(
                part(squared_early, piece, columns), part(centred_sb, piece, columns), centred_ps[:, columns], ALU.mult
            )

        def square_on_scalar(centred_ps, piece, columns=whole):
            nc.scalar.activation(part(squared_late, piece, columns), centred_ps[:, columns], ACT.Square)

        def mean_of_squares(var_ps, squared, piece, columns=whole):
            nc.tensor.matmul(var_ps[:, columns], average[:], part(squared, piece, columns), start=True, stop=True)

        def root(var_ps, piece, columns=whole):
            nc.scalar.activation(rstd[piece][:, columns], var_ps[:, columns], ACT.Abs_reciprocal_sqrt, bias=eps_cols[piece][:, 0:1])

        def normalise(centred, piece, columns=whole):
            nc.vector.scalar_tensor_tensor(
                normed[piece][:, columns], centred, gain_col[:, 0:1], rstd[piece][:, columns], ALU.mult, ALU.mult
            )

        def linear(dw_ps, piece, columns=whole):
            nc.tensor.matmul(dw_ps[:, columns], w_lin_sb[:], normed[piece][:, columns], start=True, stop=True)
            nc.scalar.activation(dws[piece][:, columns], dw_ps[:, columns], ACT.Identity, bias=both_biases[:, 0:1])

        def gate(t_ps, act_feat, piece):
            nc.tensor.matmul(t_ps[:], w_t_sb[:], part(act_feat, piece), start=True, stop=True)
            nc.scalar.activation(gates[piece][:], t_ps[:], ACT.Silu, bias=b_t_col[:, 0:1])

        def place(piece):
            piece_offsets = offsets[:, piece * (PIECE // 16) : (piece + 1) * (PIECE // 16)]
            nc.vector.tensor_tensor(window[:].indirect(piece_offsets), dws[piece][:], gates[piece][:], ALU.mult)

        first_centred_0, second_centred_0 = bank("first_a"), bank("second_a")
        centre_features(first_centred_0, wdot_0[:, first], first)
        centre_features(second_centred_0, wdot_0[:, second], second)
        nc.scalar.activation(act_feat_early[:], tfeat_early[:], ACT.Silu)
        nc.scalar.activation(act_feat_late[:], tfeat_late[:], ACT.Silu)
        copy_to_sbuf(first_centred_0, 0, first)
        copy_to_sbuf(second_centred_0, 0, second)
        square_on_vector(first_centred_0, 0, first)
        square_on_vector(second_centred_0, 0, second)
        gate(bank("first_c"), act_feat_early, 0)
        gate(bank("second_c"), act_feat_early, 1)
        first_centred_1, second_centred_1 = bank("first_b"), bank("second_b")
        centre_features(first_centred_1, wdot_1[:, first], first)
        centre_features(second_centred_1, wdot_1[:, second], second)
        copy_to_sbuf(first_centred_1, 1, first)
        copy_to_sbuf(second_centred_1, 1, second)
        square_on_vector(first_centred_1, 1, first)
        square_on_vector(second_centred_1, 1, second)

        w_lin_f32 = held.tile([P, P], F32, name="w_lin_f32")
        nc.vector.tensor_copy(w_lin_f32[:], w_lin_sb[:])
        bias_ps = bank("second_d")
        nc.tensor.matmul(bias_ps[:, 0:1], w_lin_f32[:], bias_col[:], start=True, stop=True)
        both_biases = held.tile([P, 1], F32, name="both_biases")
        nc.vector.tensor_tensor(both_biases[:], bias_ps[:, 0:1], b_lin_col[:], ALU.add)

        var_0 = bank("second_c")
        mean_of_squares(var_0, squared_early, 0, first)
        mean_of_squares(var_0, squared_early, 0, second)
        root(var_0, 0, first)
        root(var_0, 0, second)
        normalise(first_centred_0[:, first], 0, first)
        normalise(second_centred_0[:, second], 0, second)
        linear(bank("first_d"), 0, first)
        linear(bank("second_d"), 0, second)
        var_1 = bank("first_c")
        mean_of_squares(var_1, squared_early, 1, first)
        mean_of_squares(var_1, squared_early, 1, second)
        root(var_1, 1)
        normalise(first_centred_1[:, first], 1, first)
        normalise(part(centred_sb, 1, second), 1, second)
        linear(bank("first_d"), 1)
        place(0)
        first_centred_2, second_centred_2, centred_3 = bank("second_b"), bank("second_a"), bank("first_b")
        centre_features(first_centred_2, part(wdot_late, 2, first), first)
        centre_features(second_centred_2, part(wdot_late, 2, second), second)
        centre_features(centred_3, part(wdot_late, 3))
        square_on_scalar(first_centred_2, 2, first)
        square_on_scalar(second_centred_2, 2, second)
        square_on_scalar(centred_3, 3)
        var_2, var_3 = bank("first_a"), bank("first_c")
        mean_of_squares(var_2, squared_late, 2)
        mean_of_squares(var_3, squared_late, 3)
        root(var_2, 2)
        root(var_3, 3)
        normalise(first_centred_2[:, first], 2, first)
        normalise(second_centred_2[:, second], 2, second)
        place(1)
        normalise(centred_3[:], 3)
        linear(bank("first_a"), 2)
        gate(bank("second_c"), act_feat_late, 2)
        place(2)
        gate(bank("second_c"), act_feat_late, 3)
        linear(bank("first_a"), 3)
        place(3)

        nc.sync.dma_start(out, window[:])
